import numpy as np
import ml_dtypes


def mxq(x, axis, fmt="e4m3"):
    dtype, down = {"e4m3": (ml_dtypes.float8_e4m3fn, 7), "e5m2": (ml_dtypes.float8_e5m2, 14)}[fmt]
    v = np.moveaxis(np.asarray(x, np.float32).astype(ml_dtypes.bfloat16).astype(np.float64), axis, -1)
    blocks = v.reshape(v.shape[:-1] + (-1, 32))
    amax = np.abs(blocks).max(-1, keepdims=True)
    byte = np.maximum(np.where(amax > 0, np.frexp(amax)[1] - 1 + 127, 0) - down, 1)
    scale = np.exp2(byte - 127.0)
    codes = (blocks / scale).astype(np.float32).astype(dtype).astype(np.float64)
    return np.moveaxis((codes * scale).reshape(v.shape), -1, axis)


WIDE = False


def mx_kscale(k):
    if not WIDE:
        return np.ones(k)
    levels = np.array([10, -10, 5, -5, 0])
    if k % 512:
        return np.exp2(np.random.permutation(np.resize(levels, k // 32))).repeat(32)
    a = np.empty((k // 512, 16))
    for p in range(k // 512):
        a[p, :8] = np.random.permutation(np.resize(levels, 8))
        for g in range(8):
            far = levels[np.abs(levels - a[p, g]) >= 10]
            a[p, g + 8] = far[np.random.randint(len(far))]
    return np.exp2(a.ravel()).repeat(32)


BF16 = ml_dtypes.bfloat16


def bf(x):
    return np.asarray(x, np.float32).astype(BF16)


def f64(x):
    return np.asarray(x).astype(np.float64)


B, T, D, H = 4, 256, 512, 2048
N = B * T
EMA0 = 1.0


def sigmoid(v):
    return 1.0 / (1.0 + np.exp(-v))


def surprise_gate(err):
    err_mag = np.sqrt(np.sum(err * err)) / N
    ema = 0.95 * EMA0 + 0.05 * err_mag
    return np.minimum(err_mag / np.maximum(ema, 1e-8), 3.0)


def draw0():
    s, t = mx_kscale(D), mx_kscale(N)
    return {"err": bf(np.random.standard_normal((N, D)) * 2.3 * s[None, :] * t[:, None]),
            "W_down": bf(np.random.standard_normal((D, H)) / np.sqrt(D) / s[:, None]),
            "gate_pre": bf(np.random.standard_normal((N, H))),
            "up_pre": bf(np.random.standard_normal((N, H))),
            "x_pred": bf(np.random.standard_normal((N, D)) / t[:, None])}


def core(err, W_down, gate_pre, up_pre, x_pred):
    err, gate_pre, up_pre = f64(err), f64(gate_pre), f64(up_pre)
    sg = surprise_gate(err)
    d_h = mxq(err, 1, "e4m3") @ mxq(f64(W_down), 0, "e4m3")
    sig = sigmoid(gate_pre)
    gate_act = gate_pre * sig
    d_gate_act = d_h * up_pre
    d_up_val = d_h * gate_act
    d_gate_pre = d_gate_act * sig * (1.0 + gate_pre * (1.0 - sig))
    xq = mxq(f64(x_pred), 0, "e4m3")
    grad_gate = (mxq(d_gate_pre, 0, "e4m3").T @ xq) / N
    grad_up = (mxq(d_up_val, 0, "e4m3").T @ xq) / N
    return grad_up * sg, grad_gate * sg


def e4m3fn_bytes(y):
    return np.clip(np.asarray(y, np.float64), -448.0, 448.0).astype(np.float32).astype(ml_dtypes.float8_e4m3fn).view(np.uint8)


def e4m3fn_values(b):
    return np.asarray(b, np.uint8).view(ml_dtypes.float8_e4m3fn).astype(np.float64)


def setup_inputs():
    d = draw0()
    x0 = np.asarray(d['W_down']).astype(np.float64)
    s = (np.max(np.abs(x0), axis=(1,), keepdims=True) / 448.0).astype(np.float32)
    out = {}
    for k, v in d.items():
        if k == 'W_down':
            out['W_down_bytes'] = e4m3fn_bytes(x0 / s.astype(np.float64))
            out['W_down_scale'] = s
        else:
            out[k] = v
    return out


def reference(err, W_down_bytes, W_down_scale, gate_pre, up_pre, x_pred):
    return core(err, e4m3fn_values(W_down_bytes) * W_down_scale.astype(np.float64), gate_pre, up_pre, x_pred)

@@ -1,0 +1,369 @@
+from contextlib import ExitStack
+
+import concourse.mybir as mybir
+from concourse.masks import make_identity
+
+N, D, H = 1024, 512, 2048
+FLOPS = 2 * N * D * H * 3
+
+F32 = mybir.dt.float32
+BF16 = mybir.dt.bfloat16
+U32 = mybir.dt.uint32
+U8 = mybir.dt.uint8
+X4 = mybir.dt.float8_e4m3fn_x4
+FP8 = mybir.dt.float8_e4m3fn
+ACT = mybir.ActivationFunctionType
+ALU = mybir.AluOpType
+
+P = 128
+T4 = 4
+NG = 2
+HT = 128
+NT = H // HT
+CHUNKS = (256,256,512,512,512)
+WLOADS = (256,256,512,512,512)
+WP = 256
+GATE_ON_GPSIMD = True
+UP_PE_FROM = 1
+LOOK = 3
+
+
+def tile_continuummemorysystem_pa_kernel(tc, err, W_down_bytes, W_down_scale, gate_pre, up_pre, x_pred, out_0, out_1):
+    nc = tc.nc
+    with ExitStack() as ctx:
+        keep = ctx.enter_context(tc.tile_pool(name="keep", bufs=1))
+        wpool = ctx.enter_context(tc.tile_pool(name="wpool", bufs=2))
+        work = ctx.enter_context(tc.tile_pool(name="work", bufs=2))
+        psum = ctx.enter_context(tc.psum_pool(name="psum", bufs=1))
+        ctx.enter_context(tc.manual_schedule())
+
+        w_scale = keep.tile([P, T4], F32, name="w_scale")
+        nc.sync.dma_start(out=w_scale[:], in_=W_down_scale.rearrange("(p t) o -> p (t o)", t=T4))
+        w_view = W_down_bytes.rearrange("(p t) n -> p t n", t=T4)
+        w_bytes = []
+        w0 = 0
+
+        def load_w(width, start):
+            tile = keep.tile([P, T4, width], U8, name="w_bytes%d" % start)
+            nc.sync.dma_start(out=tile[:], in_=w_view[:, :, start:start + width])
+            w_bytes.append((start, width, tile))
+
+        load_w(WLOADS[0], 0)
+        w0 = WLOADS[0]
+        e_view = err.rearrange("(g m t) k -> g m t k", g=NG, t=T4)
+        e_raw = []
+        for g in range(NG):
+            et = keep.tile([P, T4, D], BF16, name="e_raw%d" % g)
+            nc.sync.dma_start(out=et[:], in_=e_view[g])
+            e_raw.append(et)
+        g_view = gate_pre.rearrange("(g p t) h -> g p t h", g=NG, t=T4)
+        u_view = up_pre.rearrange("(g p t) h -> g p t h", g=NG, t=T4)
+        chunks = []
+
+        def load_chunk(c0, width):
+            gt = keep.tile([P, NG, T4, width], BF16, name="gate_in%d" % c0)
+            ut = keep.tile([P, NG, T4, width], BF16, name="up_in%d" % c0)
+            for g in range(NG):
+                nc.sync.dma_start(out=gt[:, g], in_=g_view[g][:, :, c0:c0 + width])
+            for g in range(NG):
+                nc.sync.dma_start(out=ut[:, g], in_=u_view[g][:, :, c0:c0 + width])
+            chunks.append((c0, width, gt, ut))
+
+        load_chunk(0, CHUNKS[0])
+        x_view = x_pred.rearrange("(g p t) d -> g p t d", g=NG, t=T4)
+        x_raw = keep.tile([P, NG, T4, D], BF16, name="x_raw")
+        load_w(WLOADS[1], w0)
+        w0 += WLOADS[1]
+        for g in range(NG):
+            nc.sync.dma_start(out=x_raw[:, g], in_=x_view[g])
+        c0 = CHUNKS[0]
+        for i in range(1, len(CHUNKS)):
+            load_chunk(c0, CHUNKS[i])
+            c0 += CHUNKS[i]
+            if i + 1 < len(WLOADS):
+                load_w(WLOADS[i + 1], w0)
+                w0 += WLOADS[i + 1]
+
+        def chunk_cols(i):
+            col = i * HT
+            for start, width, gt, ut in chunks:
+                if start <= col < start + width:
+                    return gt, ut, slice(col - start, col - start + HT)
+
+        half = keep.tile([P, 1], F32, name="half")
+        nc.gpsimd.memset(half[:], 0.5)
+        warm = keep.tile([P, 1], F32, name="warm")
+        nc.scalar.activation(out=warm[:], in_=half[:], func=ACT.Silu)
+        ident = keep.tile([P, P], F32, name="ident")
+        make_identity(nc, ident[:])
+        ident_bf = keep.tile([P, P], BF16, name="ident_bf")
+        make_identity(nc, ident_bf[:])
+        ones = keep.tile([P, P], F32, name="ones")
+        nc.gpsimd.memset(ones[:], 1.0)
+        minus1 = keep.tile([P, 1], F32, name="minus1")
+        nc.gpsimd.memset(minus1[:], -1.0)
+
+        w_codes = keep.tile([P, H], U32, name="w_codes", align_bytes=64)
+        w_exp = keep.tile([P, H], U8, name="w_exp", align_bytes=64)
+        w_wide, w_lace = {}, {}
+
+        def w_widen(j):
+            col = j * WP
+            wide = wpool.tile([P, T4, WP], BF16, tag="w_wide", name="w_wide%d" % j)
+            w_wide[j] = wide
+            for start, width, tile in w_bytes:
+                if start <= col < start + width:
+                    for t in range(T4):
+                        nc.scalar.activation(
+                            out=wide[:, t, :],
+                            in_=tile[:, t, col - start:col - start + WP].bitcast(FP8),
+                            func=ACT.Copy, scale=w_scale[:, t:t + 1])
+
+        def w_interleave(j):
+            lace = wpool.tile([P, WP, T4], BF16, tag="w_lace", align_bytes=64, name="w_lace%d" % j)
+            w_lace[j] = lace
+            nc.vector.tensor_copy(out=lace[:], in_=w_wide[j][:].rearrange("p t n -> p n t"))
+
+        def w_quant(j):
+            cols = slice(j * WP, (j + 1) * WP)
+            nc.vector.quantize_mx(out=w_codes[:, cols].bitcast(X4), scales=w_exp[:, cols],
+                                  in_=w_lace[j][:].rearrange("p n t -> p (n t)"))
+
+        e_lace = [keep.tile([P, T4 * P * T4], BF16, name="e_lace%d" % g, align_bytes=64) for g in range(NG)]
+        e_codes = keep.tile([P, NG * T4 * P], U32, name="e_codes", align_bytes=64)
+        e_exp = keep.tile([P, NG * T4 * P], U8, name="e_exp", align_bytes=64)
+        e_ps = {}
+
+        def e_transpose(g):
+            words = e_raw[g][:].rearrange("p t k -> p (t k)").bitcast(F32)
+            for b in range(2):
+                xt = psum.tile([P, 2, 2, P], F32, tag="dh", bufs=4, name="e_ps%d%d" % (g, b))
+                e_ps[g, b] = xt
+                for tt in range(2):
+                    t = 2 * b + tt
+                    for u in range(2):
+                        nc.tensor.transpose(xt[:, tt, u, :], words[:, 256 * t + u:256 * (t + 1):2], ident[:])
+
+        def e_copy(g, b):
+            dst = e_lace[g][:].bitcast(F32)[:, 512 * b:512 * (b + 1)].rearrange("p (t m u) -> p t m u", t=2, u=2)
+            src = e_ps[g, b][:].rearrange("p t u m -> p t m u")
+            if b == 0:
+                nc.vector.tensor_copy(out=dst, in_=src)
+            else:
+                nc.scalar.copy(out=dst, in_=src)
+
+        def e_quant(g):
+            cols = slice(g * 512, (g + 1) * 512)
+            nc.vector.quantize_mx(out=e_codes[:, cols].bitcast(X4), scales=e_exp[:, cols], in_=e_lace[g][:])
+
+        gram = psum.tile([P, P], F32, tag="o", bufs=2, name="gram")
+
+        def e_gram(g):
+            for t in range(T4):
+                for kb in range(D // P):
+                    blk = e_raw[g][:, t, kb * P:(kb + 1) * P]
+                    nc.tensor.matmul(gram[:], lhsT=blk, rhs=blk,
+                                     start=(g == 0 and t == 0 and kb == 0),
+                                     stop=(g == NG - 1 and t == T4 - 1 and kb == D // P - 1))
+
+        diag = keep.tile([P, 1], F32, name="diag")
+        diag_all = keep.tile([P, P], F32, name="diag_all")
+        mean_sq = keep.tile([P, 1], F32, name="mean_sq")
+        s_up = keep.tile([P, 1], F32, name="s_up")
+        s_gate = keep.tile([P, 1], F32, name="s_gate")
+        total = psum.tile([P, 1], F32, tag="o", bufs=2, name="total")
+
+        def gram_diag():
+            nc.vector.scalar_tensor_tensor(out=diag_all[:], in0=gram[:], scalar=1.0, in1=ident[:],
+                                           op0=ALU.mult, op1=ALU.mult, accum_out=diag[:])
+
+        def gram_total():
+            nc.tensor.matmul(total[:], lhsT=ones[:], rhs=diag[:], start=True, stop=True)
+
+        def gram_mean():
+            nc.vector.tensor_scalar(out=mean_sq[:], in0=total[:], scalar1=1.0 / (N * N), scalar2=None, op0=ALU.mult)
+
+        def surprise():
+            em = keep.tile([P, 1], F32, name="em")
+            nc.gpsimd.tensor_tensor(out=em[:], in0=mean_sq[:], in1=half[:], op=ALU.pow)
+            ema = keep.tile([P, 1], F32, name="ema")
+            nc.gpsimd.tensor_scalar(out=ema[:], in0=em[:], scalar1=0.05, scalar2=0.95, op0=ALU.mult, op1=ALU.add)
+            inv = keep.tile([P, 1], F32, name="inv")
+            nc.gpsimd.tensor_tensor(out=inv[:], in0=ema[:], in1=minus1[:], op=ALU.pow)
+            sg = keep.tile([P, 1], F32, name="sg")
+            nc.gpsimd.tensor_tensor(out=sg[:], in0=em[:], in1=inv[:], op=ALU.mult)
+            nc.gpsimd.tensor_scalar(out=s_up[:], in0=sg[:], scalar1=3.0, scalar2=0.5 / N, op0=ALU.min, op1=ALU.mult)
+            nc.gpsimd.tensor_scalar(out=s_gate[:], in0=s_up[:], scalar1=-1.0, scalar2=0.0, op0=ALU.mult, op1=ALU.add)
+
+        x_lace = keep.tile([P, NG, D, T4], BF16, name="x_lace", align_bytes=64)
+        x_codes = keep.tile([P, NG, D], U32, name="x_codes", align_bytes=64)
+        x_exp = keep.tile([P, NG, D], U8, name="x_exp", align_bytes=64)
+
+        def x_interleave(g):
+            nc.vector.tensor_copy(out=x_lace[:, g], in_=x_raw[:, g].rearrange("p t d -> p d t"))
+
+        def x_quant(g):
+            nc.vector.quantize_mx(out=x_codes[:, g].bitcast(X4), scales=x_exp[:, g],
+                                  in_=x_lace[:, g].rearrange("p d t -> p (d t)"))
+
+        T, Z, W2, A, UPS, DH, DU, DG, QU, QG, O = {}, {}, {}, {}, {}, {}, {}, {}, {}, {}, {}
+        SH = [P, NG, HT, T4]
+
+        def scalar_t(i):
+            if i >= NT:
+                return
+            gt, ut, cols = chunk_cols(i)
+            T[i] = work.tile(SH, F32, tag="tanh", bufs=LOOK + 1, name="tanh%d" % i)
+            nc.scalar.activation(out=T[i][:], in_=gt[:, :, :, cols].rearrange("p g t h -> p g h t"), func=ACT.Tanh, scale=0.5)
+
+        def scalar_z(i):
+            if i >= NT:
+                return
+            gt, ut, cols = chunk_cols(i)
+            Z[i] = work.tile(SH, F32, tag="silu", bufs=LOOK + 1, name="silu%d" % i)
+            nc.scalar.activation(out=Z[i][:], in_=gt[:, :, :, cols].rearrange("p g t h -> p g h t"), func=ACT.Silu, scale=-1.0)
+
+        def pe_up(i):
+            if i >= NT or i < UP_PE_FROM:
+                return
+            gt, ut, cols = chunk_cols(i)
+            for g in range(NG):
+                ps = psum.tile([P, T4, HT], F32, tag="up", bufs=2, name="up_ps%d_%d" % (i, g))
+                UPS[i, g] = ps
+                nc.tensor.matmul(ps[:], lhsT=ident_bf[:], rhs=ut[:, g, :, cols], start=True, stop=True)
+
+        def pe_stage1(i):
+            if i >= NT:
+                return
+            cols = slice(i * HT, (i + 1) * HT)
+            for g in range(NG):
+                ps = psum.tile([P, T4, HT], F32, tag="dh", bufs=4, name="dh%d_%d" % (i, g))
+                DH[i, g] = ps
+                for t in range(T4):
+                    m = slice((g * T4 + t) * P, (g * T4 + t + 1) * P)
+                    nc.tensor.matmul_mx(out=ps[:, t, :], lhsT=e_codes[:, m].bitcast(X4), lhsT_scale=e_exp[:, m],
+                                        rhs=w_codes[:, cols].bitcast(X4), rhs_scale=w_exp[:, cols],
+                                        start=True, stop=True)
+
+        def vec_w(i):
+            if i >= NT:
+                return
+            gt, ut, cols = chunk_cols(i)
+            W2[i] = work.tile(SH, F32, tag="w2", bufs=2, name="w2_%d" % i)
+            for g in range(NG):
+                src = ut[:, g, :, cols] if i < UP_PE_FROM else UPS[i, g][:]
+                nc.vector.scalar_tensor_tensor(out=W2[i][:, g], in0=Z[i][:, g], scalar=1.0,
+                                               in1=src.rearrange("p t h -> p h t"), op0=ALU.subtract, op1=ALU.mult)
+
+        def vec_a(i):
+            if i >= NT:
+                return
+            A[i] = work.tile(SH, F32, tag="a", bufs=2, name="a%d" % i)
+            for g in range(NG):
+                nc.vector.scalar_tensor_tensor(out=A[i][:, g], in0=T[i][:, g], scalar=1.0,
+                                               in1=DH[i, g][:].rearrange("p t h -> p h t"), op0=ALU.add, op1=ALU.mult)
+
+        def vec_dup(i):
+            gt, ut, cols = chunk_cols(i)
+            DU[i] = work.tile(SH, BF16, tag="du", bufs=2, align_bytes=64, name="du%d" % i)
+            nc.vector.tensor_tensor(out=DU[i][:], in0=A[i][:], in1=gt[:, :, :, cols].rearrange("p g t h -> p g h t"), op=ALU.mult)
+
+        def dgate(i):
+            DG[i] = work.tile(SH, BF16, tag="dg", bufs=1, align_bytes=64, name="dg%d" % i)
+            eng = nc.gpsimd if GATE_ON_GPSIMD else nc.vector
+            eng.tensor_tensor(out=DG[i][:], in0=A[i][:], in1=W2[i][:], op=ALU.mult)
+
+        def quant(i, src, dst, tag):
+            codes = work.tile([P, NG, HT], U32, tag=tag + "c", bufs=3, align_bytes=64, name="%sc%d" % (tag, i))
+            exps = work.tile([P, NG, HT], U8, tag=tag + "s", bufs=3, align_bytes=64, name="%ss%d" % (tag, i))
+            nc.vector.quantize_mx(out=codes[:].rearrange("p g h -> p (g h)").bitcast(X4),
+                                  scales=exps[:].rearrange("p g h -> p (g h)"),
+                                  in_=src[i][:].rearrange("p g h t -> p (g h t)"))
+            dst[i] = (codes, exps)
+
+        def pe_stage2(i):
+            if i < 0:
+                return
+            for k, q in enumerate((QU, QG)):
+                ps = psum.tile([P, D], F32, tag="o", bufs=2, name="o%d_%d" % (i, k))
+                O[i, k] = ps
+                codes, exps = q[i]
+                for g in range(NG):
+                    nc.tensor.matmul_mx(out=ps[:], lhsT=codes[:, g].bitcast(X4), lhsT_scale=exps[:, g],
+                                        rhs=x_codes[:, g].bitcast(X4), rhs_scale=x_exp[:, g],
+                                        start=(g == 0), stop=(g == NG - 1))
+
+        def evac(i, k):
+            if i < 0:
+                return
+            res = work.tile([P, D], F32, tag="res%d" % k, bufs=3, name="res%d_%d" % (i, k))
+            nc.scalar.activation(out=res[:], in_=O[i, k][:], func=ACT.Copy, scale=(s_up, s_gate)[k][:])
+            nc.sync.dma_start(out=(out_0, out_1)[k][i * HT:(i + 1) * HT, :], in_=res[:])
+
+        w_widen(0)
+        e_transpose(0)
+        e_transpose(1)
+        e_gram(0)
+        e_copy(0, 1)
+        e_copy(1, 1)
+        w_interleave(0)
+        w_quant(0)
+        e_copy(0, 0)
+        e_quant(0)
+        e_copy(1, 0)
+        e_quant(1)
+        scalar_t(0)
+        scalar_z(0)
+        pe_stage1(0)
+        e_gram(1)
+        pe_up(0)
+        pe_up(1)
+        pe_stage1(1)
+        vec_a(0)
+        vec_w(0)
+        gram_diag()
+        gram_total()
+        scalar_t(1)
+        scalar_z(1)
+        w_widen(1)
+        w_interleave(1)
+        w_quant(1)
+        for i in range(2, LOOK):
+            scalar_t(i)
+            scalar_z(i)
+
+        for i in range(NT):
+            pe_stage2(i - 1)
+            scalar_t(i + LOOK)
+            evac(i - 1, 0)
+            scalar_z(i + LOOK)
+            evac(i - 1, 1)
+            if i % 2 == 0 and i // 2 + 2 < H // WP:
+                w_widen(i // 2 + 2)
+            dgate_now = GATE_ON_GPSIMD
+            if dgate_now:
+                dgate(i)
+            vec_w(i + 1)
+            pe_up(i + 2)
+            vec_a(i + 1)
+            vec_dup(i)
+            if i == 0:
+                gram_mean()
+                surprise()
+                for g in range(NG):
+                    x_interleave(g)
+            if not dgate_now:
+                dgate(i)
+            if i == 0:
+                for g in range(NG):
+                    x_quant(g)
+            if i % 2 == 1 and (i + 3) // 2 < H // WP:
+                w_interleave((i + 3) // 2)
+            quant(i, DG, QG, "qg") if dgate_now else quant(i, DU, QU, "qu")
+            quant(i, DU, QU, "qu") if dgate_now else quant(i, DG, QG, "qg")
+            if i % 2 == 1 and (i + 3) // 2 < H // WP:
+                w_quant((i + 3) // 2)
+            pe_stage1(i + 2)
+        pe_stage2(NT - 1)
+        evac(NT - 1, 0)
+        evac(NT - 1, 1)

@@ -22,10 +22,11 @@ HT = 128
 NT = H // HT
 CHUNKS = (256,256,512,512,512)
 WLOADS = (256,256,512,512,512)
-WP = 256
+WP = 128
 GATE_ON_GPSIMD = True
 UP_PE_FROM = 1
 LOOK = 3
+LOAD_ORDER = "w0 g0 e0 e1 u0 x0 x1 w1 g1 u1 w2 g2 u2 w3 g3 u3 w4 g4 u4".split()
 
 
 def tile_continuummemorysystem_pa_kernel(tc, err, W_down_bytes, W_down_scale, gate_pre, up_pre, x_pred, out_0, out_1):
@@ -41,48 +42,37 @@ def tile_continuummemorysystem_pa_kernel(tc, err, W_down_bytes, W_down_scale, ga
         nc.sync.dma_start(out=w_scale[:], in_=W_down_scale.rearrange("(p t) o -> p (t o)", t=T4))
         w_view = W_down_bytes.rearrange("(p t) n -> p t n", t=T4)
         w_bytes = []
-        w0 = 0
 
         def load_w(width, start):
             tile = keep.tile([P, T4, width], U8, name="w_bytes%d" % start)
             nc.sync.dma_start(out=tile[:], in_=w_view[:, :, start:start + width])
             w_bytes.append((start, width, tile))
 
-        load_w(WLOADS[0], 0)
-        w0 = WLOADS[0]
         e_view = err.rearrange("(g m t) k -> g m t k", g=NG, t=T4)
-        e_raw = []
-        for g in range(NG):
-            et = keep.tile([P, T4, D], BF16, name="e_raw%d" % g)
-            nc.sync.dma_start(out=et[:], in_=e_view[g])
-            e_raw.append(et)
+        e_raw = [keep.tile([P, T4, D], BF16, name="e_raw%d" % g) for g in range(NG)]
+        x_view = x_pred.rearrange("(g p t) d -> g p t d", g=NG, t=T4)
+        x_raw = keep.tile([P, NG, T4, D], BF16, name="x_raw")
         g_view = gate_pre.rearrange("(g p t) h -> g p t h", g=NG, t=T4)
         u_view = up_pre.rearrange("(g p t) h -> g p t h", g=NG, t=T4)
         chunks = []
-
-        def load_chunk(c0, width):
-            gt = keep.tile([P, NG, T4, width], BF16, name="gate_in%d" % c0)
-            ut = keep.tile([P, NG, T4, width], BF16, name="up_in%d" % c0)
-            for g in range(NG):
-                nc.sync.dma_start(out=gt[:, g], in_=g_view[g][:, :, c0:c0 + width])
-            for g in range(NG):
-                nc.sync.dma_start(out=ut[:, g], in_=u_view[g][:, :, c0:c0 + width])
-            chunks.append((c0, width, gt, ut))
-
-        load_chunk(0, CHUNKS[0])
-        x_view = x_pred.rearrange("(g p t) d -> g p t d", g=NG, t=T4)
-        x_raw = keep.tile([P, NG, T4, D], BF16, name="x_raw")
-        load_w(WLOADS[1], w0)
-        w0 += WLOADS[1]
-        for g in range(NG):
-            nc.sync.dma_start(out=x_raw[:, g], in_=x_view[g])
-        c0 = CHUNKS[0]
-        for i in range(1, len(CHUNKS)):
-            load_chunk(c0, CHUNKS[i])
-            c0 += CHUNKS[i]
-            if i + 1 < len(WLOADS):
-                load_w(WLOADS[i + 1], w0)
-                w0 += WLOADS[i + 1]
+        c0 = 0
+        for width in CHUNKS:
+            chunks.append((c0, width, keep.tile([P, NG, T4, width], BF16, name="gate_in%d" % c0),
+                           keep.tile([P, NG, T4, width], BF16, name="up_in%d" % c0)))
+            c0 += width
+        for item in LOAD_ORDER:
+            kind, n = item[0], int(item[1:])
+            if kind == "w":
+                load_w(WLOADS[n], sum(WLOADS[:n]))
+            elif kind == "e":
+                nc.sync.dma_start(out=e_raw[n][:], in_=e_view[n])
+            elif kind == "x":
+                nc.sync.dma_start(out=x_raw[:, n], in_=x_view[n])
+            else:
+                start, width, gt, ut = chunks[n]
+                for g in range(NG):
+                    dst, view = (gt, g_view) if kind == "g" else (ut, u_view)
+                    nc.sync.dma_start(out=dst[:, g], in_=view[g][:, :, start:start + width])
 
         def chunk_cols(i):
             col = i * HT
@@ -144,13 +134,13 @@ def tile_continuummemorysystem_pa_kernel(tc, err, W_down_bytes, W_down_scale, ga
                     for u in range(2):
                         nc.tensor.transpose(xt[:, tt, u, :], words[:, 256 * t + u:256 * (t + 1):2], ident[:])
 
-        def e_copy(g, b):
+        def e_copy(g, b, on_scalar):
             dst = e_lace[g][:].bitcast(F32)[:, 512 * b:512 * (b + 1)].rearrange("p (t m u) -> p t m u", t=2, u=2)
             src = e_ps[g, b][:].rearrange("p t u m -> p t m u")
-            if b == 0:
-                nc.vector.tensor_copy(out=dst, in_=src)
-            else:
+            if on_scalar:
                 nc.scalar.copy(out=dst, in_=src)
+            else:
+                nc.vector.tensor_copy(out=dst, in_=src)
 
         def e_quant(g):
             cols = slice(g * 512, (g + 1) * 512)
@@ -199,8 +189,14 @@ def tile_continuummemorysystem_pa_kernel(tc, err, W_down_bytes, W_down_scale, ga
         x_codes = keep.tile([P, NG, D], U32, name="x_codes", align_bytes=64)
         x_exp = keep.tile([P, NG, D], U8, name="x_exp", align_bytes=64)
 
-        def x_interleave(g):
-            nc.vector.tensor_copy(out=x_lace[:, g], in_=x_raw[:, g].rearrange("p t d -> p d t"))
+        def x_interleave(g, eng):
+            src = x_raw[:, g].rearrange("p t d -> p d t")
+            if eng == "g":
+                nc.gpsimd.tensor_scalar(out=x_lace[:, g], in0=src, scalar1=1.0, scalar2=0.0, op0=ALU.mult, op1=ALU.add)
+            elif eng == "s":
+                nc.scalar.copy(out=x_lace[:, g], in_=src)
+            else:
+                nc.vector.tensor_copy(out=x_lace[:, g], in_=src)
 
         def x_quant(g):
             nc.vector.quantize_mx(out=x_codes[:, g].bitcast(X4), scales=x_exp[:, g],
@@ -268,9 +264,8 @@ def tile_continuummemorysystem_pa_kernel(tc, err, W_down_bytes, W_down_scale, ga
             DU[i] = work.tile(SH, BF16, tag="du", bufs=2, align_bytes=64, name="du%d" % i)
             nc.vector.tensor_tensor(out=DU[i][:], in0=A[i][:], in1=gt[:, :, :, cols].rearrange("p g t h -> p g h t"), op=ALU.mult)
 
-        def dgate(i):
+        def dgate(i, eng):
             DG[i] = work.tile(SH, BF16, tag="dg", bufs=1, align_bytes=64, name="dg%d" % i)
-            eng = nc.gpsimd if GATE_ON_GPSIMD else nc.vector
             eng.tensor_tensor(out=DG[i][:], in0=A[i][:], in1=W2[i][:], op=ALU.mult)
 
         def quant(i, src, dst, tag):
@@ -301,69 +296,288 @@ def tile_continuummemorysystem_pa_kernel(tc, err, W_down_bytes, W_down_scale, ga
             nc.sync.dma_start(out=(out_0, out_1)[k][i * HT:(i + 1) * HT, :], in_=res[:])
 
         w_widen(0)
+        w_widen(1)
         e_transpose(0)
         e_transpose(1)
         e_gram(0)
-        e_copy(0, 1)
-        e_copy(1, 1)
-        w_interleave(0)
-        w_quant(0)
-        e_copy(0, 0)
-        e_quant(0)
-        e_copy(1, 0)
-        e_quant(1)
         scalar_t(0)
         scalar_z(0)
+        w_interleave(0)
+        w_quant(0)
+        w_interleave(1)
+        w_quant(1)
+        e_copy(0, 0, False)
+        e_copy(0, 1, True)
+        e_quant(0)
+        e_copy(1, 0, False)
+        e_copy(1, 1, True)
+        e_quant(1)
         pe_stage1(0)
-        e_gram(1)
         pe_up(0)
         pe_up(1)
         pe_stage1(1)
-        vec_a(0)
-        vec_w(0)
-        gram_diag()
-        gram_total()
+        e_gram(1)
         scalar_t(1)
         scalar_z(1)
-        w_widen(1)
-        w_interleave(1)
-        w_quant(1)
-        for i in range(2, LOOK):
-            scalar_t(i)
-            scalar_z(i)
-
-        for i in range(NT):
-            pe_stage2(i - 1)
-            scalar_t(i + LOOK)
-            evac(i - 1, 0)
-            scalar_z(i + LOOK)
-            evac(i - 1, 1)
-            if i % 2 == 0 and i // 2 + 2 < H // WP:
-                w_widen(i // 2 + 2)
-            dgate_now = GATE_ON_GPSIMD
-            if dgate_now:
-                dgate(i)
-            vec_w(i + 1)
-            pe_up(i + 2)
-            vec_a(i + 1)
-            vec_dup(i)
-            if i == 0:
-                gram_mean()
-                surprise()
-                for g in range(NG):
-                    x_interleave(g)
-            if not dgate_now:
-                dgate(i)
-            if i == 0:
-                for g in range(NG):
-                    x_quant(g)
-            if i % 2 == 1 and (i + 3) // 2 < H // WP:
-                w_interleave((i + 3) // 2)
-            quant(i, DG, QG, "qg") if dgate_now else quant(i, DU, QU, "qu")
-            quant(i, DU, QU, "qu") if dgate_now else quant(i, DG, QG, "qg")
-            if i % 2 == 1 and (i + 3) // 2 < H // WP:
-                w_quant((i + 3) // 2)
-            pe_stage1(i + 2)
-        pe_stage2(NT - 1)
-        evac(NT - 1, 0)
-        evac(NT - 1, 1)
+        vec_w(0)
+        vec_a(0)
+        x_interleave(0, "s")
+        scalar_t(2)
+        scalar_z(2)
+        w_widen(2)
+        scalar_t(3)
+        scalar_z(3)
+        dgate(0, nc.gpsimd)
+        vec_w(1)
+        pe_up(2)
+        vec_a(1)
+        gram_diag()
+        gram_total()
+        vec_dup(0)
+        x_interleave(1, "v")
+        gram_mean()
+        surprise()
+        w_interleave(2)
+        quant(0, DU, QU, "qu")
+        w_quant(2)
+        x_quant(0)
+        x_quant(1)
+        quant(0, DG, QG, "qg")
+        pe_stage1(2)
+        pe_stage2(0)
+        w_widen(3)
+        scalar_t(4)
+        evac(0, 0)
+        scalar_z(4)
+        evac(0, 1)
+        dgate(1, nc.gpsimd)
+        vec_w(2)
+        pe_up(3)
+        vec_a(2)
+        vec_dup(1)
+        w_interleave(3)
+        quant(1, DU, QU, "qu")
+        w_quant(3)
+        quant(1, DG, QG, "qg")
+        pe_stage1(3)
+        pe_stage2(1)
+        w_widen(4)
+        scalar_t(5)
+        evac(1, 0)
+        scalar_z(5)
+        evac(1, 1)
+        dgate(2, nc.gpsimd)
+        vec_w(3)
+        pe_up(4)
+        vec_a(3)
+        vec_dup(2)
+        w_interleave(4)
+        quant(2, DU, QU, "qu")
+        w_quant(4)
+        quant(2, DG, QG, "qg")
+        pe_stage1(4)
+        pe_stage2(2)
+        w_widen(5)
+        scalar_t(6)
+        evac(2, 0)
+        scalar_z(6)
+        evac(2, 1)
+        dgate(3, nc.gpsimd)
+        vec_w(4)
+        pe_up(5)
+        vec_a(4)
+        vec_dup(3)
+        w_interleave(5)
+        quant(3, DU, QU, "qu")
+        w_quant(5)
+        quant(3, DG, QG, "qg")
+        pe_stage1(5)
+        pe_stage2(3)
+        w_widen(6)
+        scalar_t(7)
+        evac(3, 0)
+        scalar_z(7)
+        evac(3, 1)
+        dgate(4, nc.gpsimd)
+        vec_w(5)
+        pe_up(6)
+        vec_a(5)
+        vec_dup(4)
+        w_interleave(6)
+        quant(4, DU, QU, "qu")
+        w_quant(6)
+        quant(4, DG, QG, "qg")
+        pe_stage1(6)
+        pe_stage2(4)
+        w_widen(7)
+        scalar_t(8)
+        evac(4, 0)
+        scalar_z(8)
+        evac(4, 1)
+        dgate(5, nc.gpsimd)
+        vec_w(6)
+        pe_up(7)
+        vec_a(6)
+        vec_dup(5)
+        w_interleave(7)
+        quant(5, DU, QU, "qu")
+        w_quant(7)
+        quant(5, DG, QG, "qg")
+        pe_stage1(7)
+        pe_stage2(5)
+        w_widen(8)
+        scalar_t(9)
+        evac(5, 0)
+        scalar_z(9)
+        evac(5, 1)
+        dgate(6, nc.gpsimd)
+        vec_w(7)
+        pe_up(8)
+        vec_a(7)
+        vec_dup(6)
+        w_interleave(8)
+        quant(6, DU, QU, "qu")
+        w_quant(8)
+        quant(6, DG, QG, "qg")
+        pe_stage1(8)
+        pe_stage2(6)
+        w_widen(9)
+        scalar_t(10)
+        evac(6, 0)
+        scalar_z(10)
+        evac(6, 1)
+        dgate(7, nc.gpsimd)
+        vec_w(8)
+        pe_up(9)
+        vec_a(8)
+        vec_dup(7)
+        w_interleave(9)
+        quant(7, DU, QU, "qu")
+        w_quant(9)
+        quant(7, DG, QG, "qg")
+        pe_stage1(9)
+        pe_stage2(7)
+        w_widen(10)
+        scalar_t(11)
+        evac(7, 0)
+        scalar_z(11)
+        evac(7, 1)
+        dgate(8, nc.gpsimd)
+        vec_w(9)
+        pe_up(10)
+        vec_a(9)
+        vec_dup(8)
+        w_interleave(10)
+        quant(8, DU, QU, "qu")
+        w_quant(10)
+        quant(8, DG, QG, "qg")
+        pe_stage1(10)
+        pe_stage2(8)
+        w_widen(11)
+        scalar_t(12)
+        evac(8, 0)
+        scalar_z(12)
+        evac(8, 1)
+        dgate(9, nc.gpsimd)
+        vec_w(10)
+        pe_up(11)
+        vec_a(10)
+        vec_dup(9)
+        w_interleave(11)
+        quant(9, DU, QU, "qu")
+        w_quant(11)
+        quant(9, DG, QG, "qg")
+        pe_stage1(11)
+        pe_stage2(9)
+        w_widen(12)
+        scalar_t(13)
+        evac(9, 0)
+        scalar_z(13)
+        evac(9, 1)
+        dgate(10, nc.gpsimd)
+        vec_w(11)
+        pe_up(12)
+        vec_a(11)
+        vec_dup(10)
+        w_interleave(12)
+        quant(10, DU, QU, "qu")
+        w_quant(12)
+        quant(10, DG, QG, "qg")
+        pe_stage1(12)
+        pe_stage2(10)
+        w_widen(13)
+        scalar_t(14)
+        evac(10, 0)
+        scalar_z(14)
+        evac(10, 1)
+        dgate(11, nc.gpsimd)
+        vec_w(12)
+        pe_up(13)
+        vec_a(12)
+        vec_dup(11)
+        w_interleave(13)
+        quant(11, DU, QU, "qu")
+        w_quant(13)
+        quant(11, DG, QG, "qg")
+        pe_stage1(13)
+        pe_stage2(11)
+        w_widen(14)
+        scalar_t(15)
+        evac(11, 0)
+        scalar_z(15)
+        evac(11, 1)
+        dgate(12, nc.gpsimd)
+        vec_w(13)
+        pe_up(14)
+        vec_a(13)
+        vec_dup(12)
+        w_interleave(14)
+        quant(12, DU, QU, "qu")
+        w_quant(14)
+        quant(12, DG, QG, "qg")
+        pe_stage1(14)
+        pe_stage2(12)
+        w_widen(15)
+        scalar_t(16)
+        evac(12, 0)
+        scalar_z(16)
+        evac(12, 1)
+        dgate(13, nc.gpsimd)
+        vec_w(14)
+        pe_up(15)
+        vec_a(14)
+        vec_dup(13)
+        w_interleave(15)
+        quant(13, DU, QU, "qu")
+        w_quant(15)
+        quant(13, DG, QG, "qg")
+        pe_stage1(15)
+        pe_stage2(13)
+        scalar_t(17)
+        evac(13, 0)
+        scalar_z(17)
+        evac(13, 1)
+        dgate(14, nc.gpsimd)
+        vec_w(15)
+        pe_up(16)
+        vec_a(15)
+        vec_dup(14)
+        quant(14, DU, QU, "qu")
+        quant(14, DG, QG, "qg")
+        pe_stage1(16)
+        pe_stage2(14)
+        scalar_t(18)
+        evac(14, 0)
+        scalar_z(18)
+        evac(14, 1)
+        vec_w(16)
+        pe_up(17)
+        vec_a(16)
+        vec_dup(15)
+        dgate(15, nc.vector)
+        quant(15, DU, QU, "qu")
+        quant(15, DG, QG, "qg")
+        pe_stage1(17)
+        pe_stage2(15)
+        evac(15, 0)
+        evac(15, 1)

@@ -20,13 +20,15 @@ T4 = 4
 NG = 2
 HT = 128
 NT = H // HT
-CHUNKS = (256,256,512,512,512)
-WLOADS = (256,256,512,512,512)
-WP = 128
-GATE_ON_GPSIMD = True
+CHUNKS = (256,256,256,256,256,256,256,256)
+WLOADS = (512,512,1024)
 UP_PE_FROM = 1
+UNITS = (1,1,2,2,2,2,2,2,1,1)
 LOOK = 3
-LOAD_ORDER = "w0 g0 e0 e1 u0 x0 x1 w1 g1 u1 w2 g2 u2 w3 g3 u3 w4 g4 u4".split()
+WPREP = (512,512,512,512)
+UPSTEP = False
+EVAC_ON_VECTOR = ((15, 1),)
+LOAD_ORDER = "w0 g0 e0 e1 u0 g1 u1 w1 x0 x1 g2 u2 g3 u3 w2 g4 u4 g5 u5 g6 u6 g7 u7".split()
 
 
 def tile_continuummemorysystem_pa_kernel(tc, err, W_down_bytes, W_down_scale, gate_pre, up_pre, x_pred, out_0, out_1):
@@ -49,7 +51,7 @@ def tile_continuummemorysystem_pa_kernel(tc, err, W_down_bytes, W_down_scale, ga
             w_bytes.append((start, width, tile))
 
         e_view = err.rearrange("(g m t) k -> g m t k", g=NG, t=T4)
-        e_raw = [keep.tile([P, T4, D], BF16, name="e_raw%d" % g) for g in range(NG)]
+        e_raw = [work.tile([P, T4, D], BF16, tag="dg", bufs=2, align_bytes=64, name="e_raw%d" % g) for g in range(NG)]
         x_view = x_pred.rearrange("(g p t) d -> g p t d", g=NG, t=T4)
         x_raw = keep.tile([P, NG, T4, D], BF16, name="x_raw")
         g_view = gate_pre.rearrange("(g p t) h -> g p t h", g=NG, t=T4)
@@ -98,8 +100,9 @@ def tile_continuummemorysystem_pa_kernel(tc, err, W_down_bytes, W_down_scale, ga
         w_wide, w_lace = {}, {}
 
         def w_widen(j):
-            col = j * WP
-            wide = wpool.tile([P, T4, WP], BF16, tag="w_wide", name="w_wide%d" % j)
+            WP = WPREP[j]
+            col = sum(WPREP[:j])
+            wide = wpool.tile([P, T4, WP], BF16, tag="w_wide", bufs=1, name="w_wide%d" % j)
             w_wide[j] = wide
             for start, width, tile in w_bytes:
                 if start <= col < start + width:
@@ -109,17 +112,25 @@ def tile_continuummemorysystem_pa_kernel(tc, err, W_down_bytes, W_down_scale, ga
                             in_=tile[:, t, col - start:col - start + WP].bitcast(FP8),
                             func=ACT.Copy, scale=w_scale[:, t:t + 1])
 
-        def w_interleave(j):
-            lace = wpool.tile([P, WP, T4], BF16, tag="w_lace", align_bytes=64, name="w_lace%d" % j)
+        def interleave(eng, out, in_):
+            if eng == "g":
+                nc.gpsimd.tensor_scalar(out=out, in0=in_, scalar1=1.0, scalar2=0.0, op0=ALU.mult, op1=ALU.add)
+            elif eng == "s":
+                nc.scalar.copy(out=out, in_=in_)
+            else:
+                nc.vector.tensor_copy(out=out, in_=in_)
+
+        def w_interleave(j, eng):
+            lace = wpool.tile([P, WPREP[j], T4], BF16, tag="lace", bufs=3, align_bytes=64, name="w_lace%d" % j)
             w_lace[j] = lace
-            nc.vector.tensor_copy(out=lace[:], in_=w_wide[j][:].rearrange("p t n -> p n t"))
+            interleave(eng, lace[:], w_wide[j][:].rearrange("p t n -> p n t"))
 
         def w_quant(j):
-            cols = slice(j * WP, (j + 1) * WP)
+            cols = slice(sum(WPREP[:j]), sum(WPREP[:j + 1]))
             nc.vector.quantize_mx(out=w_codes[:, cols].bitcast(X4), scales=w_exp[:, cols],
                                   in_=w_lace[j][:].rearrange("p n t -> p (n t)"))
 
-        e_lace = [keep.tile([P, T4 * P * T4], BF16, name="e_lace%d" % g, align_bytes=64) for g in range(NG)]
+        e_lace = [work.tile([P, T4 * P * T4], BF16, tag="du", bufs=2, align_bytes=64, name="e_lace%d" % g) for g in range(NG)]
         e_codes = keep.tile([P, NG * T4 * P], U32, name="e_codes", align_bytes=64)
         e_exp = keep.tile([P, NG * T4 * P], U8, name="e_exp", align_bytes=64)
         e_ps = {}
@@ -185,22 +196,18 @@ def tile_continuummemorysystem_pa_kernel(tc, err, W_down_bytes, W_down_scale, ga
             nc.gpsimd.tensor_scalar(out=s_up[:], in0=sg[:], scalar1=3.0, scalar2=0.5 / N, op0=ALU.min, op1=ALU.mult)
             nc.gpsimd.tensor_scalar(out=s_gate[:], in0=s_up[:], scalar1=-1.0, scalar2=0.0, op0=ALU.mult, op1=ALU.add)
 
-        x_lace = keep.tile([P, NG, D, T4], BF16, name="x_lace", align_bytes=64)
+        x_lace = {}
         x_codes = keep.tile([P, NG, D], U32, name="x_codes", align_bytes=64)
         x_exp = keep.tile([P, NG, D], U8, name="x_exp", align_bytes=64)
 
         def x_interleave(g, eng):
-            src = x_raw[:, g].rearrange("p t d -> p d t")
-            if eng == "g":
-                nc.gpsimd.tensor_scalar(out=x_lace[:, g], in0=src, scalar1=1.0, scalar2=0.0, op0=ALU.mult, op1=ALU.add)
-            elif eng == "s":
-                nc.scalar.copy(out=x_lace[:, g], in_=src)
-            else:
-                nc.vector.tensor_copy(out=x_lace[:, g], in_=src)
+            lace = wpool.tile([P, D, T4], BF16, tag="lace", bufs=3, align_bytes=64, name="x_lace%d" % g)
+            x_lace[g] = lace
+            interleave(eng, lace[:], x_raw[:, g].rearrange("p t d -> p d t"))
 
         def x_quant(g):
             nc.vector.quantize_mx(out=x_codes[:, g].bitcast(X4), scales=x_exp[:, g],
-                                  in_=x_lace[:, g].rearrange("p d t -> p (d t)"))
+                                  in_=x_lace[g][:].rearrange("p d t -> p (d t)"))
 
         T, Z, W2, A, UPS, DH, DU, DG, QU, QG, O = {}, {}, {}, {}, {}, {}, {}, {}, {}, {}, {}
         SH = [P, NG, HT, T4]
@@ -209,24 +216,35 @@ def tile_continuummemorysystem_pa_kernel(tc, err, W_down_bytes, W_down_scale, ga
             if i >= NT:
                 return
             gt, ut, cols = chunk_cols(i)
-            T[i] = work.tile(SH, F32, tag="tanh", bufs=LOOK + 1, name="tanh%d" % i)
+            T[i] = work.tile(SH, F32, tag="tanh", bufs=LOOK + 2, name="tanh%d" % i)
             nc.scalar.activation(out=T[i][:], in_=gt[:, :, :, cols].rearrange("p g t h -> p g h t"), func=ACT.Tanh, scale=0.5)
 
         def scalar_z(i):
             if i >= NT:
                 return
             gt, ut, cols = chunk_cols(i)
-            Z[i] = work.tile(SH, F32, tag="silu", bufs=LOOK + 1, name="silu%d" % i)
+            Z[i] = work.tile(SH, F32, tag="silu", bufs=LOOK + 2, name="silu%d" % i)
             nc.scalar.activation(out=Z[i][:], in_=gt[:, :, :, cols].rearrange("p g t h -> p g h t"), func=ACT.Silu, scale=-1.0)
+
+        unit_of = {}
+        starts = []
+        for u in range(len(UNITS)):
+            starts.append(sum(UNITS[:u]))
+            for k in range(UNITS[u]):
+                unit_of[starts[u] + k] = (u, k)
+
+        def tiles_of(u):
+            return range(starts[u], starts[u] + UNITS[u]) if 0 <= u < len(UNITS) else range(0)
 
         def pe_up(i):
             if i >= NT or i < UP_PE_FROM:
                 return
             gt, ut, cols = chunk_cols(i)
             for g in range(NG):
-                ps = psum.tile([P, T4, HT], F32, tag="up", bufs=2, name="up_ps%d_%d" % (i, g))
+                ps = psum.tile([P, HT, T4] if UPSTEP else [P, T4, HT], F32, tag="up", bufs=2, name="up_ps%d_%d" % (i, g))
                 UPS[i, g] = ps
-                nc.tensor.matmul(ps[:], lhsT=ident_bf[:], rhs=ut[:, g, :, cols], start=True, stop=True)
+                nc.tensor.matmul(ps[:].rearrange("p h t -> p t h") if UPSTEP else ps[:], lhsT=ident_bf[:],
+                                 rhs=ut[:, g, :, cols], start=True, stop=True)
 
         def pe_stage1(i):
             if i >= NT:
@@ -241,71 +259,82 @@ def tile_continuummemorysystem_pa_kernel(tc, err, W_down_bytes, W_down_scale, ga
                                         rhs=w_codes[:, cols].bitcast(X4), rhs_scale=w_exp[:, cols],
                                         start=True, stop=True)
 
+        def unit_tile(store, u, dtype, tag):
+            if u not in store:
+                store[u] = work.tile([P, NG, UNITS[u] * HT, T4], dtype, tag=tag, bufs=2, align_bytes=64, name="%s%d" % (tag, u))
+            return store[u]
+
         def vec_w(i):
-            if i >= NT:
-                return
+            u, k = unit_of[i]
             gt, ut, cols = chunk_cols(i)
-            W2[i] = work.tile(SH, F32, tag="w2", bufs=2, name="w2_%d" % i)
-            for g in range(NG):
-                src = ut[:, g, :, cols] if i < UP_PE_FROM else UPS[i, g][:]
-                nc.vector.scalar_tensor_tensor(out=W2[i][:, g], in0=Z[i][:, g], scalar=1.0,
-                                               in1=src.rearrange("p t h -> p h t"), op0=ALU.subtract, op1=ALU.mult)
+            w2 = unit_tile(W2, u, F32, "w2")
+            for g in reversed(range(NG)):
+                if i < UP_PE_FROM:
+                    src = ut[:, g, :, cols].rearrange("p t h -> p h t")
+                else:
+                    src = UPS[i, g][:] if UPSTEP else UPS[i, g][:].rearrange("p t h -> p h t")
+                nc.vector.scalar_tensor_tensor(out=w2[:, g, k * HT:(k + 1) * HT], in0=Z[i][:, g], scalar=1.0,
+                                               in1=src, op0=ALU.subtract, op1=ALU.mult)
 
         def vec_a(i):
-            if i >= NT:
-                return
-            A[i] = work.tile(SH, F32, tag="a", bufs=2, name="a%d" % i)
-            for g in range(NG):
-                nc.vector.scalar_tensor_tensor(out=A[i][:, g], in0=T[i][:, g], scalar=1.0,
+            u, k = unit_of[i]
+            a = unit_tile(A, u, F32, "a")
+            for g in reversed(range(NG)):
+                nc.vector.scalar_tensor_tensor(out=a[:, g, k * HT:(k + 1) * HT], in0=T[i][:, g], scalar=1.0,
                                                in1=DH[i, g][:].rearrange("p t h -> p h t"), op0=ALU.add, op1=ALU.mult)
 
-        def vec_dup(i):
-            gt, ut, cols = chunk_cols(i)
-            DU[i] = work.tile(SH, BF16, tag="du", bufs=2, align_bytes=64, name="du%d" % i)
-            nc.vector.tensor_tensor(out=DU[i][:], in0=A[i][:], in1=gt[:, :, :, cols].rearrange("p g t h -> p g h t"), op=ALU.mult)
+        def unit_cols(u):
+            gt, ut, cols = chunk_cols(starts[u])
+            return gt, slice(cols.start, cols.start + UNITS[u] * HT)
 
-        def dgate(i, eng):
-            DG[i] = work.tile(SH, BF16, tag="dg", bufs=1, align_bytes=64, name="dg%d" % i)
-            eng.tensor_tensor(out=DG[i][:], in0=A[i][:], in1=W2[i][:], op=ALU.mult)
+        def dup(u, eng):
+            gt, cols = unit_cols(u)
+            du = unit_tile(DU, u, BF16, "du")
+            eng.tensor_tensor(out=du[:], in0=A[u][:], in1=gt[:, :, :, cols].rearrange("p g t h -> p g h t"), op=ALU.mult)
 
-        def quant(i, src, dst, tag):
-            codes = work.tile([P, NG, HT], U32, tag=tag + "c", bufs=3, align_bytes=64, name="%sc%d" % (tag, i))
-            exps = work.tile([P, NG, HT], U8, tag=tag + "s", bufs=3, align_bytes=64, name="%ss%d" % (tag, i))
+        def dgate(u, eng):
+            dg = unit_tile(DG, u, BF16, "dg")
+            eng.tensor_tensor(out=dg[:], in0=A[u][:], in1=W2[u][:], op=ALU.mult)
+
+        def quant(u, src, dst, tag):
+            n = UNITS[u] * HT
+            codes = work.tile([P, NG, n], U32, tag=tag + "c", bufs=2, align_bytes=64, name="%sc%d" % (tag, u))
+            exps = work.tile([P, NG, n], U8, tag=tag + "s", bufs=2, align_bytes=64, name="%ss%d" % (tag, u))
             nc.vector.quantize_mx(out=codes[:].rearrange("p g h -> p (g h)").bitcast(X4),
                                   scales=exps[:].rearrange("p g h -> p (g h)"),
-                                  in_=src[i][:].rearrange("p g h t -> p (g h t)"))
-            dst[i] = (codes, exps)
+                                  in_=src[u][:].rearrange("p g h t -> p (g h t)"))
+            dst[u] = (codes, exps)
 
         def pe_stage2(i):
-            if i < 0:
-                return
-            for k, q in enumerate((QU, QG)):
-                ps = psum.tile([P, D], F32, tag="o", bufs=2, name="o%d_%d" % (i, k))
-                O[i, k] = ps
-                codes, exps = q[i]
+            u, k = unit_of[i]
+            for m, q in enumerate((QU, QG)):
+                ps = psum.tile([P, D], F32, tag="o", bufs=2, name="o%d_%d" % (i, m))
+                O[i, m] = ps
+                codes, exps = q[u]
+                cols = slice(k * HT, (k + 1) * HT)
                 for g in range(NG):
-                    nc.tensor.matmul_mx(out=ps[:], lhsT=codes[:, g].bitcast(X4), lhsT_scale=exps[:, g],
+                    nc.tensor.matmul_mx(out=ps[:], lhsT=codes[:, g, cols].bitcast(X4), lhsT_scale=exps[:, g, cols],
                                         rhs=x_codes[:, g].bitcast(X4), rhs_scale=x_exp[:, g],
                                         start=(g == 0), stop=(g == NG - 1))
 
-        def evac(i, k):
-            if i < 0:
-                return
-            res = work.tile([P, D], F32, tag="res%d" % k, bufs=3, name="res%d_%d" % (i, k))
-            nc.scalar.activation(out=res[:], in_=O[i, k][:], func=ACT.Copy, scale=(s_up, s_gate)[k][:])
-            nc.sync.dma_start(out=(out_0, out_1)[k][i * HT:(i + 1) * HT, :], in_=res[:])
+        def evac(i, m):
+            res = work.tile([P, D], F32, tag="res%d" % m, bufs=3, name="res%d_%d" % (i, m))
+            if (i, m) in EVAC_ON_VECTOR:
+                nc.vector.tensor_scalar(out=res[:], in0=O[i, m][:], scalar1=(s_up, s_gate)[m][:], scalar2=None, op0=ALU.mult)
+            else:
+                nc.scalar.activation(out=res[:], in_=O[i, m][:], func=ACT.Copy, scale=(s_up, s_gate)[m][:])
+            nc.sync.dma_start(out=(out_0, out_1)[m][i * HT:(i + 1) * HT, :], in_=res[:])
 
         w_widen(0)
-        w_widen(1)
         e_transpose(0)
         e_transpose(1)
         e_gram(0)
         scalar_t(0)
         scalar_z(0)
-        w_interleave(0)
+        w_interleave(0, "v")
         w_quant(0)
-        w_interleave(1)
-        w_quant(1)
+        pe_up(0)
+        pe_up(1)
         e_copy(0, 0, False)
         e_copy(0, 1, True)
         e_quant(0)
@@ -313,271 +342,200 @@ def tile_continuummemorysystem_pa_kernel(tc, err, W_down_bytes, W_down_scale, ga
         e_copy(1, 1, True)
         e_quant(1)
         pe_stage1(0)
-        pe_up(0)
-        pe_up(1)
         pe_stage1(1)
         e_gram(1)
         scalar_t(1)
         scalar_z(1)
+        x_interleave(0, "g")
+        x_interleave(1, "g")
         vec_w(0)
         vec_a(0)
-        x_interleave(0, "s")
+        pe_stage1(2)
+        w_widen(1)
         scalar_t(2)
         scalar_z(2)
-        w_widen(2)
         scalar_t(3)
         scalar_z(3)
+        scalar_t(4)
+        scalar_z(4)
+        scalar_t(5)
+        scalar_z(5)
         dgate(0, nc.gpsimd)
         vec_w(1)
         pe_up(2)
         vec_a(1)
+        pe_stage1(3)
         gram_diag()
         gram_total()
-        vec_dup(0)
-        x_interleave(1, "v")
+        dup(0, nc.vector)
         gram_mean()
         surprise()
-        w_interleave(2)
-        quant(0, DU, QU, "qu")
-        w_quant(2)
+        w_interleave(1, "v")
         x_quant(0)
         x_quant(1)
-        quant(0, DG, QG, "qg")
-        pe_stage1(2)
-        pe_stage2(0)
-        w_widen(3)
-        scalar_t(4)
-        evac(0, 0)
-        scalar_z(4)
-        evac(0, 1)
+        w_quant(1)
+        quant(0, DU, QU, "qu")
+        w_widen(2)
+        scalar_t(6)
+        scalar_z(6)
         dgate(1, nc.gpsimd)
+        w_interleave(2, "g")
         vec_w(2)
         pe_up(3)
         vec_a(2)
-        vec_dup(1)
-        w_interleave(3)
-        quant(1, DU, QU, "qu")
-        w_quant(3)
-        quant(1, DG, QG, "qg")
-        pe_stage1(3)
-        pe_stage2(1)
-        w_widen(4)
-        scalar_t(5)
-        evac(1, 0)
-        scalar_z(5)
-        evac(1, 1)
-        dgate(2, nc.gpsimd)
+        pe_stage1(4)
         vec_w(3)
         pe_up(4)
         vec_a(3)
-        vec_dup(2)
-        w_interleave(4)
-        quant(2, DU, QU, "qu")
-        w_quant(4)
-        quant(2, DG, QG, "qg")
-        pe_stage1(4)
-        pe_stage2(2)
-        w_widen(5)
-        scalar_t(6)
-        evac(2, 0)
-        scalar_z(6)
-        evac(2, 1)
-        dgate(3, nc.gpsimd)
+        pe_stage1(5)
+        quant(0, DG, QG, "qg")
+        pe_stage2(0)
+        evac(0, 0)
+        evac(0, 1)
+        dup(1, nc.vector)
+        quant(1, DU, QU, "qu")
+        scalar_t(7)
+        scalar_z(7)
+        scalar_t(8)
+        scalar_z(8)
+        dgate(2, nc.gpsimd)
         vec_w(4)
         pe_up(5)
         vec_a(4)
-        vec_dup(3)
-        w_interleave(5)
-        quant(3, DU, QU, "qu")
-        w_quant(5)
-        quant(3, DG, QG, "qg")
-        pe_stage1(5)
-        pe_stage2(3)
-        w_widen(6)
-        scalar_t(7)
-        evac(3, 0)
-        scalar_z(7)
-        evac(3, 1)
-        dgate(4, nc.gpsimd)
+        pe_stage1(6)
         vec_w(5)
         pe_up(6)
         vec_a(5)
-        vec_dup(4)
-        w_interleave(6)
-        quant(4, DU, QU, "qu")
-        w_quant(6)
-        quant(4, DG, QG, "qg")
-        pe_stage1(6)
-        pe_stage2(4)
-        w_widen(7)
-        scalar_t(8)
-        evac(4, 0)
-        scalar_z(8)
-        evac(4, 1)
-        dgate(5, nc.gpsimd)
+        pe_stage1(7)
+        quant(1, DG, QG, "qg")
+        pe_stage2(1)
+        evac(1, 0)
+        evac(1, 1)
+        dup(2, nc.vector)
+        w_quant(2)
+        quant(2, DU, QU, "qu")
+        w_widen(3)
+        scalar_t(9)
+        scalar_z(9)
+        scalar_t(10)
+        scalar_z(10)
+        dgate(3, nc.gpsimd)
+        w_interleave(3, "g")
         vec_w(6)
         pe_up(7)
         vec_a(6)
-        vec_dup(5)
-        w_interleave(7)
-        quant(5, DU, QU, "qu")
-        w_quant(7)
-        quant(5, DG, QG, "qg")
-        pe_stage1(7)
-        pe_stage2(5)
-        w_widen(8)
-        scalar_t(9)
-        evac(5, 0)
-        scalar_z(9)
-        evac(5, 1)
-        dgate(6, nc.gpsimd)
+        pe_stage1(8)
         vec_w(7)
         pe_up(8)
         vec_a(7)
-        vec_dup(6)
-        w_interleave(8)
-        quant(6, DU, QU, "qu")
-        w_quant(8)
-        quant(6, DG, QG, "qg")
-        pe_stage1(8)
-        pe_stage2(6)
-        w_widen(9)
-        scalar_t(10)
-        evac(6, 0)
-        scalar_z(10)
-        evac(6, 1)
-        dgate(7, nc.gpsimd)
+        pe_stage1(9)
+        quant(2, DG, QG, "qg")
+        pe_stage2(2)
+        evac(2, 0)
+        evac(2, 1)
+        pe_stage2(3)
+        evac(3, 0)
+        evac(3, 1)
+        dup(3, nc.vector)
+        quant(3, DU, QU, "qu")
+        scalar_t(11)
+        scalar_z(11)
+        scalar_t(12)
+        scalar_z(12)
+        dgate(4, nc.gpsimd)
+        dup(4, nc.gpsimd)
         vec_w(8)
         pe_up(9)
         vec_a(8)
-        vec_dup(7)
-        w_interleave(9)
-        quant(7, DU, QU, "qu")
-        w_quant(9)
-        quant(7, DG, QG, "qg")
-        pe_stage1(9)
-        pe_stage2(7)
-        w_widen(10)
-        scalar_t(11)
-        evac(7, 0)
-        scalar_z(11)
-        evac(7, 1)
-        dgate(8, nc.gpsimd)
+        pe_stage1(10)
         vec_w(9)
         pe_up(10)
         vec_a(9)
-        vec_dup(8)
-        w_interleave(10)
-        quant(8, DU, QU, "qu")
-        w_quant(10)
-        quant(8, DG, QG, "qg")
-        pe_stage1(10)
-        pe_stage2(8)
-        w_widen(11)
-        scalar_t(12)
-        evac(8, 0)
-        scalar_z(12)
-        evac(8, 1)
-        dgate(9, nc.gpsimd)
+        pe_stage1(11)
+        quant(3, DG, QG, "qg")
+        pe_stage2(4)
+        evac(4, 0)
+        evac(4, 1)
+        pe_stage2(5)
+        evac(5, 0)
+        evac(5, 1)
+        w_quant(3)
+        scalar_t(13)
+        scalar_z(13)
+        scalar_t(14)
+        scalar_z(14)
+        dgate(5, nc.gpsimd)
         vec_w(10)
         pe_up(11)
         vec_a(10)
-        vec_dup(9)
-        w_interleave(11)
-        quant(9, DU, QU, "qu")
-        w_quant(11)
-        quant(9, DG, QG, "qg")
-        pe_stage1(11)
-        pe_stage2(9)
-        w_widen(12)
-        scalar_t(13)
-        evac(9, 0)
-        scalar_z(13)
-        evac(9, 1)
-        dgate(10, nc.gpsimd)
+        pe_stage1(12)
         vec_w(11)
         pe_up(12)
         vec_a(11)
-        vec_dup(10)
-        w_interleave(12)
-        quant(10, DU, QU, "qu")
-        w_quant(12)
-        quant(10, DG, QG, "qg")
-        pe_stage1(12)
-        pe_stage2(10)
-        w_widen(13)
-        scalar_t(14)
-        evac(10, 0)
-        scalar_z(14)
-        evac(10, 1)
-        dgate(11, nc.gpsimd)
+        pe_stage1(13)
+        quant(4, DU, QU, "qu")
+        quant(4, DG, QG, "qg")
+        pe_stage2(6)
+        evac(6, 0)
+        evac(6, 1)
+        pe_stage2(7)
+        evac(7, 0)
+        evac(7, 1)
+        dup(5, nc.vector)
+        quant(5, DU, QU, "qu")
+        scalar_t(15)
+        scalar_z(15)
+        dgate(6, nc.gpsimd)
+        dup(6, nc.gpsimd)
         vec_w(12)
         pe_up(13)
         vec_a(12)
-        vec_dup(11)
-        w_interleave(13)
-        quant(11, DU, QU, "qu")
-        w_quant(13)
-        quant(11, DG, QG, "qg")
-        pe_stage1(13)
-        pe_stage2(11)
-        w_widen(14)
-        scalar_t(15)
-        evac(11, 0)
-        scalar_z(15)
-        evac(11, 1)
-        dgate(12, nc.gpsimd)
+        pe_stage1(14)
         vec_w(13)
         pe_up(14)
         vec_a(13)
-        vec_dup(12)
-        w_interleave(14)
-        quant(12, DU, QU, "qu")
-        w_quant(14)
-        quant(12, DG, QG, "qg")
-        pe_stage1(14)
-        pe_stage2(12)
-        w_widen(15)
-        scalar_t(16)
-        evac(12, 0)
-        scalar_z(16)
-        evac(12, 1)
-        dgate(13, nc.gpsimd)
+        pe_stage1(15)
+        quant(5, DG, QG, "qg")
+        pe_stage2(8)
+        evac(8, 0)
+        evac(8, 1)
+        pe_stage2(9)
+        evac(9, 0)
+        evac(9, 1)
+        dgate(7, nc.gpsimd)
         vec_w(14)
         pe_up(15)
         vec_a(14)
-        vec_dup(13)
-        w_interleave(15)
-        quant(13, DU, QU, "qu")
-        w_quant(15)
-        quant(13, DG, QG, "qg")
-        pe_stage1(15)
-        pe_stage2(13)
-        scalar_t(17)
-        evac(13, 0)
-        scalar_z(17)
-        evac(13, 1)
-        dgate(14, nc.gpsimd)
+        quant(6, DU, QU, "qu")
+        quant(6, DG, QG, "qg")
+        pe_stage2(10)
+        evac(10, 0)
+        evac(10, 1)
+        pe_stage2(11)
+        evac(11, 0)
+        evac(11, 1)
+        dup(7, nc.vector)
+        quant(7, DU, QU, "qu")
+        dgate(8, nc.gpsimd)
         vec_w(15)
-        pe_up(16)
         vec_a(15)
-        vec_dup(14)
-        quant(14, DU, QU, "qu")
-        quant(14, DG, QG, "qg")
-        pe_stage1(16)
+        quant(7, DG, QG, "qg")
+        pe_stage2(12)
+        evac(12, 0)
+        evac(12, 1)
+        pe_stage2(13)
+        evac(13, 0)
+        evac(13, 1)
+        dup(8, nc.vector)
+        quant(8, DU, QU, "qu")
+        quant(8, DG, QG, "qg")
         pe_stage2(14)
-        scalar_t(18)
         evac(14, 0)
-        scalar_z(18)
         evac(14, 1)
-        vec_w(16)
-        pe_up(17)
-        vec_a(16)
-        vec_dup(15)
-        dgate(15, nc.vector)
-        quant(15, DU, QU, "qu")
-        quant(15, DG, QG, "qg")
-        pe_stage1(17)
+        dup(9, nc.vector)
+        dgate(9, nc.vector)
+        quant(9, DU, QU, "qu")
+        quant(9, DG, QG, "qg")
         pe_stage2(15)
         evac(15, 0)
         evac(15, 1)

@@ -20,15 +20,16 @@ T4 = 4
 NG = 2
 HT = 128
 NT = H // HT
-CHUNKS = (256,256,256,256,256,256,256,256)
+CHUNKS = (256,256,512,512,512)
 WLOADS = (512,512,1024)
 UP_PE_FROM = 1
 UNITS = (1,1,2,2,2,2,2,2,1,1)
-LOOK = 3
+LOOK = 2
 WPREP = (512,512,512,512)
 UPSTEP = False
 EVAC_ON_VECTOR = ((15, 1),)
-LOAD_ORDER = "w0 g0 e0 e1 u0 g1 u1 w1 x0 x1 g2 u2 g3 u3 w2 g4 u4 g5 u5 g6 u6 g7 u7".split()
+WIDEN_ON_VECTOR = ((0, 2), (0, 3),)
+LOAD_ORDER = "w0 g0 e0 e1 u0 x0 x1 w1 g1 u1 g2 u2 w2 g3 u3 g4 u4".split()
 
 
 def tile_continuummemorysystem_pa_kernel(tc, err, W_down_bytes, W_down_scale, gate_pre, up_pre, x_pred, out_0, out_1):
@@ -51,7 +52,8 @@ def tile_continuummemorysystem_pa_kernel(tc, err, W_down_bytes, W_down_scale, ga
             w_bytes.append((start, width, tile))
 
         e_view = err.rearrange("(g m t) k -> g m t k", g=NG, t=T4)
-        e_raw = [work.tile([P, T4, D], BF16, tag="dg", bufs=2, align_bytes=64, name="e_raw%d" % g) for g in range(NG)]
+        e_all = work.tile([P, NG, T4, D], BF16, tag="dd", bufs=2, align_bytes=64, name="e_all")
+        e_raw = [e_all[:, g] for g in range(NG)]
         x_view = x_pred.rearrange("(g p t) d -> g p t d", g=NG, t=T4)
         x_raw = keep.tile([P, NG, T4, D], BF16, name="x_raw")
         g_view = gate_pre.rearrange("(g p t) h -> g p t h", g=NG, t=T4)
@@ -67,7 +69,7 @@ def tile_continuummemorysystem_pa_kernel(tc, err, W_down_bytes, W_down_scale, ga
             if kind == "w":
                 load_w(WLOADS[n], sum(WLOADS[:n]))
             elif kind == "e":
-                nc.sync.dma_start(out=e_raw[n][:], in_=e_view[n])
+                nc.sync.dma_start(out=e_raw[n], in_=e_view[n])
             elif kind == "x":
                 nc.sync.dma_start(out=x_raw[:, n], in_=x_view[n])
             else:
@@ -107,10 +109,11 @@ def tile_continuummemorysystem_pa_kernel(tc, err, W_down_bytes, W_down_scale, ga
             for start, width, tile in w_bytes:
                 if start <= col < start + width:
                     for t in range(T4):
-                        nc.scalar.activation(
-                            out=wide[:, t, :],
-                            in_=tile[:, t, col - start:col - start + WP].bitcast(FP8),
-                            func=ACT.Copy, scale=w_scale[:, t:t + 1])
+                        src = tile[:, t, col - start:col - start + WP].bitcast(FP8)
+                        if (j, t) in WIDEN_ON_VECTOR:
+                            nc.vector.tensor_scalar(out=wide[:, t, :], in0=src, scalar1=w_scale[:, t:t + 1], scalar2=None, op0=ALU.mult)
+                        else:
+                            nc.scalar.activation(out=wide[:, t, :], in_=src, func=ACT.Copy, scale=w_scale[:, t:t + 1])
 
         def interleave(eng, out, in_):
             if eng == "g":
@@ -121,7 +124,7 @@ def tile_continuummemorysystem_pa_kernel(tc, err, W_down_bytes, W_down_scale, ga
                 nc.vector.tensor_copy(out=out, in_=in_)
 
         def w_interleave(j, eng):
-            lace = wpool.tile([P, WPREP[j], T4], BF16, tag="lace", bufs=3, align_bytes=64, name="w_lace%d" % j)
+            lace = wpool.tile([P, WPREP[j], T4], BF16, tag="lace", bufs=1, align_bytes=64, name="w_lace%d" % j)
             w_lace[j] = lace
             interleave(eng, lace[:], w_wide[j][:].rearrange("p t n -> p n t"))
 
@@ -130,13 +133,14 @@ def tile_continuummemorysystem_pa_kernel(tc, err, W_down_bytes, W_down_scale, ga
             nc.vector.quantize_mx(out=w_codes[:, cols].bitcast(X4), scales=w_exp[:, cols],
                                   in_=w_lace[j][:].rearrange("p n t -> p (n t)"))
 
-        e_lace = [work.tile([P, T4 * P * T4], BF16, tag="du", bufs=2, align_bytes=64, name="e_lace%d" % g) for g in range(NG)]
+        e_lace_all = work.tile([P, NG, T4 * P * T4], BF16, tag="dd", bufs=2, align_bytes=64, name="e_lace_all")
+        e_lace = [e_lace_all[:, g] for g in range(NG)]
         e_codes = keep.tile([P, NG * T4 * P], U32, name="e_codes", align_bytes=64)
         e_exp = keep.tile([P, NG * T4 * P], U8, name="e_exp", align_bytes=64)
         e_ps = {}
 
         def e_transpose(g):
-            words = e_raw[g][:].rearrange("p t k -> p (t k)").bitcast(F32)
+            words = e_raw[g].rearrange("p t k -> p (t k)").bitcast(F32)
             for b in range(2):
                 xt = psum.tile([P, 2, 2, P], F32, tag="dh", bufs=4, name="e_ps%d%d" % (g, b))
                 e_ps[g, b] = xt
@@ -146,7 +150,7 @@ def tile_continuummemorysystem_pa_kernel(tc, err, W_down_bytes, W_down_scale, ga
                         nc.tensor.transpose(xt[:, tt, u, :], words[:, 256 * t + u:256 * (t + 1):2], ident[:])
 
         def e_copy(g, b, on_scalar):
-            dst = e_lace[g][:].bitcast(F32)[:, 512 * b:512 * (b + 1)].rearrange("p (t m u) -> p t m u", t=2, u=2)
+            dst = e_lace[g].bitcast(F32)[:, 512 * b:512 * (b + 1)].rearrange("p (t m u) -> p t m u", t=2, u=2)
             src = e_ps[g, b][:].rearrange("p t u m -> p t m u")
             if on_scalar:
                 nc.scalar.copy(out=dst, in_=src)
@@ -155,7 +159,7 @@ def tile_continuummemorysystem_pa_kernel(tc, err, W_down_bytes, W_down_scale, ga
 
         def e_quant(g):
             cols = slice(g * 512, (g + 1) * 512)
-            nc.vector.quantize_mx(out=e_codes[:, cols].bitcast(X4), scales=e_exp[:, cols], in_=e_lace[g][:])
+            nc.vector.quantize_mx(out=e_codes[:, cols].bitcast(X4), scales=e_exp[:, cols], in_=e_lace[g])
 
         gram = psum.tile([P, P], F32, tag="o", bufs=2, name="gram")
 
@@ -196,20 +200,20 @@ def tile_continuummemorysystem_pa_kernel(tc, err, W_down_bytes, W_down_scale, ga
             nc.gpsimd.tensor_scalar(out=s_up[:], in0=sg[:], scalar1=3.0, scalar2=0.5 / N, op0=ALU.min, op1=ALU.mult)
             nc.gpsimd.tensor_scalar(out=s_gate[:], in0=s_up[:], scalar1=-1.0, scalar2=0.0, op0=ALU.mult, op1=ALU.add)
 
-        x_lace = {}
         x_codes = keep.tile([P, NG, D], U32, name="x_codes", align_bytes=64)
         x_exp = keep.tile([P, NG, D], U8, name="x_exp", align_bytes=64)
 
+        x_lace = keep.tile([P, NG, D, T4], BF16, name="x_lace", align_bytes=64)
+
         def x_interleave(g, eng):
-            lace = wpool.tile([P, D, T4], BF16, tag="lace", bufs=3, align_bytes=64, name="x_lace%d" % g)
-            x_lace[g] = lace
-            interleave(eng, lace[:], x_raw[:, g].rearrange("p t d -> p d t"))
+            interleave(eng, x_lace[:, g], x_raw[:, g].rearrange("p t d -> p d t"))
 
-        def x_quant(g):
-            nc.vector.quantize_mx(out=x_codes[:, g].bitcast(X4), scales=x_exp[:, g],
-                                  in_=x_lace[g][:].rearrange("p d t -> p (d t)"))
+        def x_quant():
+            nc.vector.quantize_mx(out=x_codes[:].rearrange("p g d -> p (g d)").bitcast(X4),
+                                  scales=x_exp[:].rearrange("p g d -> p (g d)"),
+                                  in_=x_lace[:].rearrange("p g d t -> p (g d t)"))
 
-        T, Z, W2, A, UPS, DH, DU, DG, QU, QG, O = {}, {}, {}, {}, {}, {}, {}, {}, {}, {}, {}
+        T, Z, W2, A, UPS, DH, DD, Q, O = {}, {}, {}, {}, {}, {}, {}, {}, {}
         SH = [P, NG, HT, T4]
 
         def scalar_t(i):
@@ -287,38 +291,43 @@ def tile_continuummemorysystem_pa_kernel(tc, err, W_down_bytes, W_down_scale, ga
             gt, ut, cols = chunk_cols(starts[u])
             return gt, slice(cols.start, cols.start + UNITS[u] * HT)
 
+        def dd_tile(u):
+            if u not in DD:
+                DD[u] = work.tile([P, 2, NG, UNITS[u] * HT, T4], BF16, tag="dd", bufs=2, align_bytes=64, name="dd%d" % u)
+            return DD[u]
+
         def dup(u, eng):
             gt, cols = unit_cols(u)
-            du = unit_tile(DU, u, BF16, "du")
-            eng.tensor_tensor(out=du[:], in0=A[u][:], in1=gt[:, :, :, cols].rearrange("p g t h -> p g h t"), op=ALU.mult)
+            eng.tensor_tensor(out=dd_tile(u)[:, 0], in0=A[u][:], in1=gt[:, :, :, cols].rearrange("p g t h -> p g h t"), op=ALU.mult)
 
         def dgate(u, eng):
-            dg = unit_tile(DG, u, BF16, "dg")
-            eng.tensor_tensor(out=dg[:], in0=A[u][:], in1=W2[u][:], op=ALU.mult)
+            eng.tensor_tensor(out=dd_tile(u)[:, 1], in0=A[u][:], in1=W2[u][:], op=ALU.mult)
 
-        def quant(u, src, dst, tag):
+        def quant(u, which):
             n = UNITS[u] * HT
-            codes = work.tile([P, NG, n], U32, tag=tag + "c", bufs=2, align_bytes=64, name="%sc%d" % (tag, u))
-            exps = work.tile([P, NG, n], U8, tag=tag + "s", bufs=2, align_bytes=64, name="%ss%d" % (tag, u))
-            nc.vector.quantize_mx(out=codes[:].rearrange("p g h -> p (g h)").bitcast(X4),
-                                  scales=exps[:].rearrange("p g h -> p (g h)"),
-                                  in_=src[u][:].rearrange("p g h t -> p (g h t)"))
-            dst[u] = (codes, exps)
+            if u not in Q:
+                codes = work.tile([P, 2, NG, n], U32, tag="qc", bufs=2, align_bytes=64, name="qc%d" % u)
+                exps = work.tile([P, 2, NG, n], U8, tag="qs", bufs=2, align_bytes=64, name="qs%d" % u)
+                Q[u] = (codes, exps)
+            codes, exps = Q[u]
+            nc.vector.quantize_mx(out=codes[:, which].rearrange("p m g h -> p (m g h)").bitcast(X4),
+                                  scales=exps[:, which].rearrange("p m g h -> p (m g h)"),
+                                  in_=DD[u][:, which].rearrange("p m g h t -> p (m g h t)"))
 
-        def pe_stage2(i):
+        def pe_stage2(i, ms):
             u, k = unit_of[i]
-            for m, q in enumerate((QU, QG)):
+            codes, exps = Q[u]
+            for m in ms:
                 ps = psum.tile([P, D], F32, tag="o", bufs=2, name="o%d_%d" % (i, m))
                 O[i, m] = ps
-                codes, exps = q[u]
                 cols = slice(k * HT, (k + 1) * HT)
                 for g in range(NG):
-                    nc.tensor.matmul_mx(out=ps[:], lhsT=codes[:, g, cols].bitcast(X4), lhsT_scale=exps[:, g, cols],
+                    nc.tensor.matmul_mx(out=ps[:], lhsT=codes[:, m, g, cols].bitcast(X4), lhsT_scale=exps[:, m, g, cols],
                                         rhs=x_codes[:, g].bitcast(X4), rhs_scale=x_exp[:, g],
                                         start=(g == 0), stop=(g == NG - 1))
 
         def evac(i, m):
-            res = work.tile([P, D], F32, tag="res%d" % m, bufs=3, name="res%d_%d" % (i, m))
+            res = work.tile([P, D], F32, tag="res%d" % m, bufs=4, name="res%d_%d" % (i, m))
             if (i, m) in EVAC_ON_VECTOR:
                 nc.vector.tensor_scalar(out=res[:], in0=O[i, m][:], scalar1=(s_up, s_gate)[m][:], scalar2=None, op0=ALU.mult)
             else:
@@ -347,7 +356,6 @@ def tile_continuummemorysystem_pa_kernel(tc, err, W_down_bytes, W_down_scale, ga
         scalar_t(1)
         scalar_z(1)
         x_interleave(0, "g")
-        x_interleave(1, "g")
         vec_w(0)
         vec_a(0)
         pe_stage1(2)
@@ -358,8 +366,6 @@ def tile_continuummemorysystem_pa_kernel(tc, err, W_down_bytes, W_down_scale, ga
         scalar_z(3)
         scalar_t(4)
         scalar_z(4)
-        scalar_t(5)
-        scalar_z(5)
         dgate(0, nc.gpsimd)
         vec_w(1)
         pe_up(2)
@@ -368,18 +374,17 @@ def tile_continuummemorysystem_pa_kernel(tc, err, W_down_bytes, W_down_scale, ga
         gram_diag()
         gram_total()
         dup(0, nc.vector)
+        x_interleave(1, "v")
+        w_interleave(1, "v")
         gram_mean()
         surprise()
-        w_interleave(1, "v")
-        x_quant(0)
-        x_quant(1)
+        x_quant()
         w_quant(1)
-        quant(0, DU, QU, "qu")
         w_widen(2)
-        scalar_t(6)
-        scalar_z(6)
+        scalar_t(5)
+        scalar_z(5)
+        w_interleave(2, "s")
         dgate(1, nc.gpsimd)
-        w_interleave(2, "g")
         vec_w(2)
         pe_up(3)
         vec_a(2)
@@ -388,16 +393,15 @@ def tile_continuummemorysystem_pa_kernel(tc, err, W_down_bytes, W_down_scale, ga
         pe_up(4)
         vec_a(3)
         pe_stage1(5)
-        quant(0, DG, QG, "qg")
-        pe_stage2(0)
+        quant(0, slice(0, 2))
+        pe_stage2(0, (0, 1))
         evac(0, 0)
         evac(0, 1)
         dup(1, nc.vector)
-        quant(1, DU, QU, "qu")
+        scalar_t(6)
+        scalar_z(6)
         scalar_t(7)
         scalar_z(7)
-        scalar_t(8)
-        scalar_z(8)
         dgate(2, nc.gpsimd)
         vec_w(4)
         pe_up(5)
@@ -407,18 +411,17 @@ def tile_continuummemorysystem_pa_kernel(tc, err, W_down_bytes, W_down_scale, ga
         pe_up(6)
         vec_a(5)
         pe_stage1(7)
-        quant(1, DG, QG, "qg")
-        pe_stage2(1)
+        quant(1, slice(0, 2))
+        pe_stage2(1, (0, 1))
         evac(1, 0)
         evac(1, 1)
         dup(2, nc.vector)
         w_quant(2)
-        quant(2, DU, QU, "qu")
         w_widen(3)
+        scalar_t(8)
+        scalar_z(8)
         scalar_t(9)
         scalar_z(9)
-        scalar_t(10)
-        scalar_z(10)
         dgate(3, nc.gpsimd)
         w_interleave(3, "g")
         vec_w(6)
@@ -429,21 +432,19 @@ def tile_continuummemorysystem_pa_kernel(tc, err, W_down_bytes, W_down_scale, ga
         pe_up(8)
         vec_a(7)
         pe_stage1(9)
-        quant(2, DG, QG, "qg")
-        pe_stage2(2)
+        quant(2, slice(0, 2))
+        pe_stage2(2, (0, 1))
         evac(2, 0)
         evac(2, 1)
-        pe_stage2(3)
+        pe_stage2(3, (0, 1))
         evac(3, 0)
         evac(3, 1)
         dup(3, nc.vector)
-        quant(3, DU, QU, "qu")
+        scalar_t(10)
+        scalar_z(10)
         scalar_t(11)
         scalar_z(11)
-        scalar_t(12)
-        scalar_z(12)
         dgate(4, nc.gpsimd)
-        dup(4, nc.gpsimd)
         vec_w(8)
         pe_up(9)
         vec_a(8)
@@ -452,18 +453,19 @@ def tile_continuummemorysystem_pa_kernel(tc, err, W_down_bytes, W_down_scale, ga
         pe_up(10)
         vec_a(9)
         pe_stage1(11)
-        quant(3, DG, QG, "qg")
-        pe_stage2(4)
+        quant(3, slice(0, 2))
+        pe_stage2(4, (0, 1))
         evac(4, 0)
         evac(4, 1)
-        pe_stage2(5)
+        pe_stage2(5, (0, 1))
         evac(5, 0)
         evac(5, 1)
+        dup(4, nc.vector)
         w_quant(3)
+        scalar_t(12)
+        scalar_z(12)
         scalar_t(13)
         scalar_z(13)
-        scalar_t(14)
-        scalar_z(14)
         dgate(5, nc.gpsimd)
         vec_w(10)
         pe_up(11)
@@ -473,20 +475,19 @@ def tile_continuummemorysystem_pa_kernel(tc, err, W_down_bytes, W_down_scale, ga
         pe_up(12)
         vec_a(11)
         pe_stage1(13)
-        quant(4, DU, QU, "qu")
-        quant(4, DG, QG, "qg")
-        pe_stage2(6)
+        quant(4, slice(0, 2))
+        pe_stage2(6, (0, 1))
         evac(6, 0)
         evac(6, 1)
-        pe_stage2(7)
+        pe_stage2(7, (0, 1))
         evac(7, 0)
         evac(7, 1)
         dup(5, nc.vector)
-        quant(5, DU, QU, "qu")
+        scalar_t(14)
+        scalar_z(14)
         scalar_t(15)
         scalar_z(15)
         dgate(6, nc.gpsimd)
-        dup(6, nc.gpsimd)
         vec_w(12)
         pe_up(13)
         vec_a(12)
@@ -495,47 +496,46 @@ def tile_continuummemorysystem_pa_kernel(tc, err, W_down_bytes, W_down_scale, ga
         pe_up(14)
         vec_a(13)
         pe_stage1(15)
-        quant(5, DG, QG, "qg")
-        pe_stage2(8)
+        quant(5, slice(0, 2))
+        pe_stage2(8, (0, 1))
         evac(8, 0)
         evac(8, 1)
-        pe_stage2(9)
+        pe_stage2(9, (0, 1))
         evac(9, 0)
         evac(9, 1)
+        dup(6, nc.vector)
         dgate(7, nc.gpsimd)
         vec_w(14)
         pe_up(15)
         vec_a(14)
-        quant(6, DU, QU, "qu")
-        quant(6, DG, QG, "qg")
-        pe_stage2(10)
+        quant(6, slice(0, 2))
+        pe_stage2(10, (0, 1))
         evac(10, 0)
         evac(10, 1)
-        pe_stage2(11)
+        pe_stage2(11, (0, 1))
         evac(11, 0)
         evac(11, 1)
         dup(7, nc.vector)
-        quant(7, DU, QU, "qu")
         dgate(8, nc.gpsimd)
         vec_w(15)
         vec_a(15)
-        quant(7, DG, QG, "qg")
-        pe_stage2(12)
+        quant(7, slice(0, 2))
+        pe_stage2(12, (0, 1))
         evac(12, 0)
         evac(12, 1)
-        pe_stage2(13)
+        pe_stage2(13, (0, 1))
         evac(13, 0)
         evac(13, 1)
         dup(8, nc.vector)
-        quant(8, DU, QU, "qu")
-        quant(8, DG, QG, "qg")
-        pe_stage2(14)
+        quant(8, slice(0, 2))
+        pe_stage2(14, (0, 1))
         evac(14, 0)
         evac(14, 1)
         dup(9, nc.vector)
-        dgate(9, nc.vector)
-        quant(9, DU, QU, "qu")
-        quant(9, DG, QG, "qg")
-        pe_stage2(15)
+        quant(9, slice(0, 1))
+        pe_stage2(15, (0,))
         evac(15, 0)
+        dgate(9, nc.vector)
+        quant(9, slice(1, 2))
+        pe_stage2(15, (1,))
         evac(15, 1)

from contextlib import ExitStack

import concourse.mybir as mybir
from concourse.masks import make_identity

N, D, H = 1024, 512, 2048
FLOPS = 2 * N * D * H * 3

F32 = mybir.dt.float32
BF16 = mybir.dt.bfloat16
U32 = mybir.dt.uint32
U8 = mybir.dt.uint8
X4 = mybir.dt.float8_e4m3fn_x4
FP8 = mybir.dt.float8_e4m3fn
ACT = mybir.ActivationFunctionType
ALU = mybir.AluOpType

P = 128
T4 = 4
NG = 2
HT = 128
NT = H // HT
CHUNKS = (256,256,512,512,512)
WLOADS = (512,512,1024)
UP_PE_FROM = 1
UNITS = (1,1,2,2,2,2,2,2,1,1)
LOOK = 2
WPREP = (512,512,512,512)
UPSTEP = False
EVAC_ON_VECTOR = ((15, 1),)
WIDEN_ON_VECTOR = ((0, 2), (0, 3),)
LOAD_ORDER = "w0 g0 e0 e1 u0 x0 x1 w1 g1 u1 g2 u2 w2 g3 u3 g4 u4".split()


def tile_continuummemorysystem_pa_kernel(tc, err, W_down_bytes, W_down_scale, gate_pre, up_pre, x_pred, out_0, out_1):
    nc = tc.nc
    with ExitStack() as ctx:
        keep = ctx.enter_context(tc.tile_pool(name="keep", bufs=1))
        wpool = ctx.enter_context(tc.tile_pool(name="wpool", bufs=2))
        work = ctx.enter_context(tc.tile_pool(name="work", bufs=2))
        psum = ctx.enter_context(tc.psum_pool(name="psum", bufs=1))
        ctx.enter_context(tc.manual_schedule())

        w_scale = keep.tile([P, T4], F32, name="w_scale")
        nc.sync.dma_start(out=w_scale[:], in_=W_down_scale.rearrange("(p t) o -> p (t o)", t=T4))
        w_view = W_down_bytes.rearrange("(p t) n -> p t n", t=T4)
        w_bytes = []

        def load_w(width, start):
            tile = keep.tile([P, T4, width], U8, name="w_bytes%d" % start)
            nc.sync.dma_start(out=tile[:], in_=w_view[:, :, start:start + width])
            w_bytes.append((start, width, tile))

        e_view = err.rearrange("(g m t) k -> g m t k", g=NG, t=T4)
        e_all = work.tile([P, NG, T4, D], BF16, tag="dd", bufs=2, align_bytes=64, name="e_all")
        e_raw = [e_all[:, g] for g in range(NG)]
        x_view = x_pred.rearrange("(g p t) d -> g p t d", g=NG, t=T4)
        x_raw = keep.tile([P, NG, T4, D], BF16, name="x_raw")
        g_view = gate_pre.rearrange("(g p t) h -> g p t h", g=NG, t=T4)
        u_view = up_pre.rearrange("(g p t) h -> g p t h", g=NG, t=T4)
        chunks = []
        c0 = 0
        for width in CHUNKS:
            chunks.append((c0, width, keep.tile([P, NG, T4, width], BF16, name="gate_in%d" % c0),
                           keep.tile([P, NG, T4, width], BF16, name="up_in%d" % c0)))
            c0 += width
        for item in LOAD_ORDER:
            kind, n = item[0], int(item[1:])
            if kind == "w":
                load_w(WLOADS[n], sum(WLOADS[:n]))
            elif kind == "e":
                nc.sync.dma_start(out=e_raw[n], in_=e_view[n])
            elif kind == "x":
                nc.sync.dma_start(out=x_raw[:, n], in_=x_view[n])
            else:
                start, width, gt, ut = chunks[n]
                for g in range(NG):
                    dst, view = (gt, g_view) if kind == "g" else (ut, u_view)
                    nc.sync.dma_start(out=dst[:, g], in_=view[g][:, :, start:start + width])

        def chunk_cols(i):
            col = i * HT
            for start, width, gt, ut in chunks:
                if start <= col < start + width:
                    return gt, ut, slice(col - start, col - start + HT)

        half = keep.tile([P, 1], F32, name="half")
        nc.gpsimd.memset(half[:], 0.5)
        warm = keep.tile([P, 1], F32, name="warm")
        nc.scalar.activation(out=warm[:], in_=half[:], func=ACT.Silu)
        ident = keep.tile([P, P], F32, name="ident")
        make_identity(nc, ident[:])
        ident_bf = keep.tile([P, P], BF16, name="ident_bf")
        make_identity(nc, ident_bf[:])
        ones = keep.tile([P, P], F32, name="ones")
        nc.gpsimd.memset(ones[:], 1.0)
        minus1 = keep.tile([P, 1], F32, name="minus1")
        nc.gpsimd.memset(minus1[:], -1.0)

        w_codes = keep.tile([P, H], U32, name="w_codes", align_bytes=64)
        w_exp = keep.tile([P, H], U8, name="w_exp", align_bytes=64)
        w_wide, w_lace = {}, {}

        def w_widen(j):
            WP = WPREP[j]
            col = sum(WPREP[:j])
            wide = wpool.tile([P, T4, WP], BF16, tag="w_wide", bufs=1, name="w_wide%d" % j)
            w_wide[j] = wide
            for start, width, tile in w_bytes:
                if start <= col < start + width:
                    for t in range(T4):
                        src = tile[:, t, col - start:col - start + WP].bitcast(FP8)
                        if (j, t) in WIDEN_ON_VECTOR:
                            nc.vector.tensor_scalar(out=wide[:, t, :], in0=src, scalar1=w_scale[:, t:t + 1], scalar2=None, op0=ALU.mult)
                        else:
                            nc.scalar.activation(out=wide[:, t, :], in_=src, func=ACT.Copy, scale=w_scale[:, t:t + 1])

        def interleave(eng, out, in_):
            if eng == "g":
                nc.gpsimd.tensor_scalar(out=out, in0=in_, scalar1=1.0, scalar2=0.0, op0=ALU.mult, op1=ALU.add)
            elif eng == "s":
                nc.scalar.copy(out=out, in_=in_)
            else:
                nc.vector.tensor_copy(out=out, in_=in_)

        def w_interleave(j, eng):
            lace = wpool.tile([P, WPREP[j], T4], BF16, tag="lace", bufs=1, align_bytes=64, name="w_lace%d" % j)
            w_lace[j] = lace
            interleave(eng, lace[:], w_wide[j][:].rearrange("p t n -> p n t"))

        def w_quant(j):
            cols = slice(sum(WPREP[:j]), sum(WPREP[:j + 1]))
            nc.vector.quantize_mx(out=w_codes[:, cols].bitcast(X4), scales=w_exp[:, cols],
                                  in_=w_lace[j][:].rearrange("p n t -> p (n t)"))

        e_lace_all = work.tile([P, NG, T4 * P * T4], BF16, tag="dd", bufs=2, align_bytes=64, name="e_lace_all")
        e_lace = [e_lace_all[:, g] for g in range(NG)]
        e_codes = keep.tile([P, NG * T4 * P], U32, name="e_codes", align_bytes=64)
        e_exp = keep.tile([P, NG * T4 * P], U8, name="e_exp", align_bytes=64)
        e_ps = {}

        def e_transpose(g):
            words = e_raw[g].rearrange("p t k -> p (t k)").bitcast(F32)
            for b in range(2):
                xt = psum.tile([P, 2, 2, P], F32, tag="dh", bufs=4, name="e_ps%d%d" % (g, b))
                e_ps[g, b] = xt
                for tt in range(2):
                    t = 2 * b + tt
                    for u in range(2):
                        nc.tensor.transpose(xt[:, tt, u, :], words[:, 256 * t + u:256 * (t + 1):2], ident[:])

        def e_copy(g, b, on_scalar):
            dst = e_lace[g].bitcast(F32)[:, 512 * b:512 * (b + 1)].rearrange("p (t m u) -> p t m u", t=2, u=2)
            src = e_ps[g, b][:].rearrange("p t u m -> p t m u")
            if on_scalar:
                nc.scalar.copy(out=dst, in_=src)
            else:
                nc.vector.tensor_copy(out=dst, in_=src)

        def e_quant(g):
            cols = slice(g * 512, (g + 1) * 512)
            nc.vector.quantize_mx(out=e_codes[:, cols].bitcast(X4), scales=e_exp[:, cols], in_=e_lace[g])

        gram = psum.tile([P, P], F32, tag="o", bufs=2, name="gram")

        def e_gram(g):
            for t in range(T4):
                for kb in range(D // P):
                    blk = e_raw[g][:, t, kb * P:(kb + 1) * P]
                    nc.tensor.matmul(gram[:], lhsT=blk, rhs=blk,
                                     start=(g == 0 and t == 0 and kb == 0),
                                     stop=(g == NG - 1 and t == T4 - 1 and kb == D // P - 1))

        diag = keep.tile([P, 1], F32, name="diag")
        diag_all = keep.tile([P, P], F32, name="diag_all")
        mean_sq = keep.tile([P, 1], F32, name="mean_sq")
        s_up = keep.tile([P, 1], F32, name="s_up")
        s_gate = keep.tile([P, 1], F32, name="s_gate")
        total = psum.tile([P, 1], F32, tag="o", bufs=2, name="total")

        def gram_diag():
            nc.vector.scalar_tensor_tensor(out=diag_all[:], in0=gram[:], scalar=1.0, in1=ident[:],
                                           op0=ALU.mult, op1=ALU.mult, accum_out=diag[:])

        def gram_total():
            nc.tensor.matmul(total[:], lhsT=ones[:], rhs=diag[:], start=True, stop=True)

        def gram_mean():
            nc.vector.tensor_scalar(out=mean_sq[:], in0=total[:], scalar1=1.0 / (N * N), scalar2=None, op0=ALU.mult)

        def surprise():
            em = keep.tile([P, 1], F32, name="em")
            nc.gpsimd.tensor_tensor(out=em[:], in0=mean_sq[:], in1=half[:], op=ALU.pow)
            ema = keep.tile([P, 1], F32, name="ema")
            nc.gpsimd.tensor_scalar(out=ema[:], in0=em[:], scalar1=0.05, scalar2=0.95, op0=ALU.mult, op1=ALU.add)
            inv = keep.tile([P, 1], F32, name="inv")
            nc.gpsimd.tensor_tensor(out=inv[:], in0=ema[:], in1=minus1[:], op=ALU.pow)
            sg = keep.tile([P, 1], F32, name="sg")
            nc.gpsimd.tensor_tensor(out=sg[:], in0=em[:], in1=inv[:], op=ALU.mult)
            nc.gpsimd.tensor_scalar(out=s_up[:], in0=sg[:], scalar1=3.0, scalar2=0.5 / N, op0=ALU.min, op1=ALU.mult)
            nc.gpsimd.tensor_scalar(out=s_gate[:], in0=s_up[:], scalar1=-1.0, scalar2=0.0, op0=ALU.mult, op1=ALU.add)

        x_codes = keep.tile([P, NG, D], U32, name="x_codes", align_bytes=64)
        x_exp = keep.tile([P, NG, D], U8, name="x_exp", align_bytes=64)

        x_lace = keep.tile([P, NG, D, T4], BF16, name="x_lace", align_bytes=64)

        def x_interleave(g, eng):
            interleave(eng, x_lace[:, g], x_raw[:, g].rearrange("p t d -> p d t"))

        def x_quant():
            nc.vector.quantize_mx(out=x_codes[:].rearrange("p g d -> p (g d)").bitcast(X4),
                                  scales=x_exp[:].rearrange("p g d -> p (g d)"),
                                  in_=x_lace[:].rearrange("p g d t -> p (g d t)"))

        T, Z, W2, A, UPS, DH, DD, Q, O = {}, {}, {}, {}, {}, {}, {}, {}, {}
        SH = [P, NG, HT, T4]

        def scalar_t(i):
            if i >= NT:
                return
            gt, ut, cols = chunk_cols(i)
            T[i] = work.tile(SH, F32, tag="tanh", bufs=LOOK + 2, name="tanh%d" % i)
            nc.scalar.activation(out=T[i][:], in_=gt[:, :, :, cols].rearrange("p g t h -> p g h t"), func=ACT.Tanh, scale=0.5)

        def scalar_z(i):
            if i >= NT:
                return
            gt, ut, cols = chunk_cols(i)
            Z[i] = work.tile(SH, F32, tag="silu", bufs=LOOK + 2, name="silu%d" % i)
            nc.scalar.activation(out=Z[i][:], in_=gt[:, :, :, cols].rearrange("p g t h -> p g h t"), func=ACT.Silu, scale=-1.0)

        unit_of = {}
        starts = []
        for u in range(len(UNITS)):
            starts.append(sum(UNITS[:u]))
            for k in range(UNITS[u]):
                unit_of[starts[u] + k] = (u, k)

        def tiles_of(u):
            return range(starts[u], starts[u] + UNITS[u]) if 0 <= u < len(UNITS) else range(0)

        def pe_up(i):
            if i >= NT or i < UP_PE_FROM:
                return
            gt, ut, cols = chunk_cols(i)
            for g in range(NG):
                ps = psum.tile([P, HT, T4] if UPSTEP else [P, T4, HT], F32, tag="up", bufs=2, name="up_ps%d_%d" % (i, g))
                UPS[i, g] = ps
                nc.tensor.matmul(ps[:].rearrange("p h t -> p t h") if UPSTEP else ps[:], lhsT=ident_bf[:],
                                 rhs=ut[:, g, :, cols], start=True, stop=True)

        def pe_stage1(i):
            if i >= NT:
                return
            cols = slice(i * HT, (i + 1) * HT)
            for g in range(NG):
                ps = psum.tile([P, T4, HT], F32, tag="dh", bufs=4, name="dh%d_%d" % (i, g))
                DH[i, g] = ps
                for t in range(T4):
                    m = slice((g * T4 + t) * P, (g * T4 + t + 1) * P)
                    nc.tensor.matmul_mx(out=ps[:, t, :], lhsT=e_codes[:, m].bitcast(X4), lhsT_scale=e_exp[:, m],
                                        rhs=w_codes[:, cols].bitcast(X4), rhs_scale=w_exp[:, cols],
                                        start=True, stop=True)

        def unit_tile(store, u, dtype, tag):
            if u not in store:
                store[u] = work.tile([P, NG, UNITS[u] * HT, T4], dtype, tag=tag, bufs=2, align_bytes=64, name="%s%d" % (tag, u))
            return store[u]

        def vec_w(i):
            u, k = unit_of[i]
            gt, ut, cols = chunk_cols(i)
            w2 = unit_tile(W2, u, F32, "w2")
            for g in reversed(range(NG)):
                if i < UP_PE_FROM:
                    src = ut[:, g, :, cols].rearrange("p t h -> p h t")
                else:
                    src = UPS[i, g][:] if UPSTEP else UPS[i, g][:].rearrange("p t h -> p h t")
                nc.vector.scalar_tensor_tensor(out=w2[:, g, k * HT:(k + 1) * HT], in0=Z[i][:, g], scalar=1.0,
                                               in1=src, op0=ALU.subtract, op1=ALU.mult)

        def vec_a(i):
            u, k = unit_of[i]
            a = unit_tile(A, u, F32, "a")
            for g in reversed(range(NG)):
                nc.vector.scalar_tensor_tensor(out=a[:, g, k * HT:(k + 1) * HT], in0=T[i][:, g], scalar=1.0,
                                               in1=DH[i, g][:].rearrange("p t h -> p h t"), op0=ALU.add, op1=ALU.mult)

        def unit_cols(u):
            gt, ut, cols = chunk_cols(starts[u])
            return gt, slice(cols.start, cols.start + UNITS[u] * HT)

        def dd_tile(u):
            if u not in DD:
                DD[u] = work.tile([P, 2, NG, UNITS[u] * HT, T4], BF16, tag="dd", bufs=2, align_bytes=64, name="dd%d" % u)
            return DD[u]

        def dup(u, eng):
            gt, cols = unit_cols(u)
            eng.tensor_tensor(out=dd_tile(u)[:, 0], in0=A[u][:], in1=gt[:, :, :, cols].rearrange("p g t h -> p g h t"), op=ALU.mult)

        def dgate(u, eng):
            eng.tensor_tensor(out=dd_tile(u)[:, 1], in0=A[u][:], in1=W2[u][:], op=ALU.mult)

        def quant(u, which):
            n = UNITS[u] * HT
            if u not in Q:
                codes = work.tile([P, 2, NG, n], U32, tag="qc", bufs=2, align_bytes=64, name="qc%d" % u)
                exps = work.tile([P, 2, NG, n], U8, tag="qs", bufs=2, align_bytes=64, name="qs%d" % u)
                Q[u] = (codes, exps)
            codes, exps = Q[u]
            nc.vector.quantize_mx(out=codes[:, which].rearrange("p m g h -> p (m g h)").bitcast(X4),
                                  scales=exps[:, which].rearrange("p m g h -> p (m g h)"),
                                  in_=DD[u][:, which].rearrange("p m g h t -> p (m g h t)"))

        def pe_stage2(i, ms):
            u, k = unit_of[i]
            codes, exps = Q[u]
            for m in ms:
                ps = psum.tile([P, D], F32, tag="o", bufs=2, name="o%d_%d" % (i, m))
                O[i, m] = ps
                cols = slice(k * HT, (k + 1) * HT)
                for g in range(NG):
                    nc.tensor.matmul_mx(out=ps[:], lhsT=codes[:, m, g, cols].bitcast(X4), lhsT_scale=exps[:, m, g, cols],
                                        rhs=x_codes[:, g].bitcast(X4), rhs_scale=x_exp[:, g],
                                        start=(g == 0), stop=(g == NG - 1))

        def evac(i, m):
            res = work.tile([P, D], F32, tag="res%d" % m, bufs=4, name="res%d_%d" % (i, m))
            if (i, m) in EVAC_ON_VECTOR:
                nc.vector.tensor_scalar(out=res[:], in0=O[i, m][:], scalar1=(s_up, s_gate)[m][:], scalar2=None, op0=ALU.mult)
            else:
                nc.scalar.activation(out=res[:], in_=O[i, m][:], func=ACT.Copy, scale=(s_up, s_gate)[m][:])
            nc.sync.dma_start(out=(out_0, out_1)[m][i * HT:(i + 1) * HT, :], in_=res[:])

        w_widen(0)
        e_transpose(0)
        e_transpose(1)
        e_gram(0)
        scalar_t(0)
        scalar_z(0)
        w_interleave(0, "v")
        w_quant(0)
        pe_up(0)
        pe_up(1)
        e_copy(0, 0, False)
        e_copy(0, 1, True)
        e_quant(0)
        e_copy(1, 0, False)
        e_copy(1, 1, True)
        e_quant(1)
        pe_stage1(0)
        pe_stage1(1)
        e_gram(1)
        scalar_t(1)
        scalar_z(1)
        x_interleave(0, "g")
        vec_w(0)
        vec_a(0)
        pe_stage1(2)
        w_widen(1)
        scalar_t(2)
        scalar_z(2)
        scalar_t(3)
        scalar_z(3)
        scalar_t(4)
        scalar_z(4)
        dgate(0, nc.gpsimd)
        vec_w(1)
        pe_up(2)
        vec_a(1)
        pe_stage1(3)
        gram_diag()
        gram_total()
        dup(0, nc.vector)
        x_interleave(1, "v")
        w_interleave(1, "v")
        gram_mean()
        surprise()
        x_quant()
        w_quant(1)
        w_widen(2)
        scalar_t(5)
        scalar_z(5)
        w_interleave(2, "s")
        dgate(1, nc.gpsimd)
        vec_w(2)
        pe_up(3)
        vec_a(2)
        pe_stage1(4)
        vec_w(3)
        pe_up(4)
        vec_a(3)
        pe_stage1(5)
        quant(0, slice(0, 2))
        pe_stage2(0, (0, 1))
        evac(0, 0)
        evac(0, 1)
        dup(1, nc.vector)
        scalar_t(6)
        scalar_z(6)
        scalar_t(7)
        scalar_z(7)
        dgate(2, nc.gpsimd)
        vec_w(4)
        pe_up(5)
        vec_a(4)
        pe_stage1(6)
        vec_w(5)
        pe_up(6)
        vec_a(5)
        pe_stage1(7)
        quant(1, slice(0, 2))
        pe_stage2(1, (0, 1))
        evac(1, 0)
        evac(1, 1)
        dup(2, nc.vector)
        w_quant(2)
        w_widen(3)
        scalar_t(8)
        scalar_z(8)
        scalar_t(9)
        scalar_z(9)
        dgate(3, nc.gpsimd)
        w_interleave(3, "g")
        vec_w(6)
        pe_up(7)
        vec_a(6)
        pe_stage1(8)
        vec_w(7)
        pe_up(8)
        vec_a(7)
        pe_stage1(9)
        quant(2, slice(0, 2))
        pe_stage2(2, (0, 1))
        evac(2, 0)
        evac(2, 1)
        pe_stage2(3, (0, 1))
        evac(3, 0)
        evac(3, 1)
        dup(3, nc.vector)
        scalar_t(10)
        scalar_z(10)
        scalar_t(11)
        scalar_z(11)
        dgate(4, nc.gpsimd)
        vec_w(8)
        pe_up(9)
        vec_a(8)
        pe_stage1(10)
        vec_w(9)
        pe_up(10)
        vec_a(9)
        pe_stage1(11)
        quant(3, slice(0, 2))
        pe_stage2(4, (0, 1))
        evac(4, 0)
        evac(4, 1)
        pe_stage2(5, (0, 1))
        evac(5, 0)
        evac(5, 1)
        dup(4, nc.vector)
        w_quant(3)
        scalar_t(12)
        scalar_z(12)
        scalar_t(13)
        scalar_z(13)
        dgate(5, nc.gpsimd)
        vec_w(10)
        pe_up(11)
        vec_a(10)
        pe_stage1(12)
        vec_w(11)
        pe_up(12)
        vec_a(11)
        pe_stage1(13)
        quant(4, slice(0, 2))
        pe_stage2(6, (0, 1))
        evac(6, 0)
        evac(6, 1)
        pe_stage2(7, (0, 1))
        evac(7, 0)
        evac(7, 1)
        dup(5, nc.vector)
        scalar_t(14)
        scalar_z(14)
        scalar_t(15)
        scalar_z(15)
        dgate(6, nc.gpsimd)
        vec_w(12)
        pe_up(13)
        vec_a(12)
        pe_stage1(14)
        vec_w(13)
        pe_up(14)
        vec_a(13)
        pe_stage1(15)
        quant(5, slice(0, 2))
        pe_stage2(8, (0, 1))
        evac(8, 0)
        evac(8, 1)
        pe_stage2(9, (0, 1))
        evac(9, 0)
        evac(9, 1)
        dup(6, nc.vector)
        dgate(7, nc.gpsimd)
        vec_w(14)
        pe_up(15)
        vec_a(14)
        quant(6, slice(0, 2))
        pe_stage2(10, (0, 1))
        evac(10, 0)
        evac(10, 1)
        pe_stage2(11, (0, 1))
        evac(11, 0)
        evac(11, 1)
        dup(7, nc.vector)
        dgate(8, nc.gpsimd)
        vec_w(15)
        vec_a(15)
        quant(7, slice(0, 2))
        pe_stage2(12, (0, 1))
        evac(12, 0)
        evac(12, 1)
        pe_stage2(13, (0, 1))
        evac(13, 0)
        evac(13, 1)
        dup(8, nc.vector)
        quant(8, slice(0, 2))
        pe_stage2(14, (0, 1))
        evac(14, 0)
        evac(14, 1)
        dup(9, nc.vector)
        quant(9, slice(0, 1))
        pe_stage2(15, (0,))
        evac(15, 0)
        dgate(9, nc.vector)
        quant(9, slice(1, 2))
        pe_stage2(15, (1,))
        evac(15, 1)
